import numpy as np
import ml_dtypes


def mxq(x, axis, fmt="e4m3"):
    dtype, down = {"e4m3": (ml_dtypes.float8_e4m3fn, 7), "e5m2": (ml_dtypes.float8_e5m2, 14)}[fmt]
    v = np.moveaxis(np.asarray(x, np.float32).astype(ml_dtypes.bfloat16).astype(np.float64), axis, -1)
    blocks = v.reshape(v.shape[:-1] + (-1, 32))
    amax = np.abs(blocks).max(-1, keepdims=True)
    byte = np.maximum(np.where(amax > 0, np.frexp(amax)[1] - 1 + 127, 0) - down, 1)
    scale = np.exp2(byte - 127.0)
    codes = (blocks / scale).astype(np.float32).astype(dtype).astype(np.float64)
    return np.moveaxis((codes * scale).reshape(v.shape), -1, axis)


WIDE = False


def mx_kscale(k):
    if not WIDE:
        return np.ones(k)
    levels = np.array([10, -10, 5, -5, 0])
    if k % 512:
        return np.exp2(np.random.permutation(np.resize(levels, k // 32))).repeat(32)
    a = np.empty((k // 512, 16))
    for p in range(k // 512):
        a[p, :8] = np.random.permutation(np.resize(levels, 8))
        for g in range(8):
            far = levels[np.abs(levels - a[p, g]) >= 10]
            a[p, g + 8] = far[np.random.randint(len(far))]
    return np.exp2(a.ravel()).repeat(32)


BF16 = ml_dtypes.bfloat16


def bf(x):
    return np.asarray(x, np.float32).astype(BF16)


def f64(x):
    return np.asarray(x).astype(np.float64)


N, D_IN, D_HID, D_OUT = 1024, 1025, 4097, 1025
K = D_IN - 1
M = D_HID - 1
EPS = 1e-7
MAX_TAN_NORM = 10.0


def arccosh(v):
    return np.log(v + np.sqrt(v * v - 1.0))


def cosh(v):
    return 0.5 * (np.exp(v) + np.exp(-v))


def sinh(v):
    return 0.5 * (np.exp(v) - np.exp(-v))


def setup_inputs():
    s = mx_kscale(K)
    c = np.sqrt(np.mean(s * s))
    g = np.random.standard_normal((N, K)) * s
    r = np.random.uniform(2.0, 4.0, (N, 1))
    xs = sinh(r) * g / np.sqrt(np.sum(g * g, axis=1, keepdims=True))
    col = np.concatenate([np.ones(1), c / s])
    return {"x_hyp": bf(np.concatenate([cosh(r), xs], axis=1)),
            "W": bf(np.random.standard_normal((D_HID, D_IN)) * 2.8 / np.sqrt(M) * col[None, :]),
            "b": bf(np.random.standard_normal(D_HID) * 3.0 / np.sqrt(M))}


def reference(x_hyp, W, b):
    x = f64(x_hyp)
    x0, xs = x[:, :1], x[:, 1:]
    d = arccosh(np.maximum(x0, 1.0 + EPS))
    ns = np.maximum(np.sqrt(np.sum(xs * xs, axis=1, keepdims=True)), EPS)
    ts = d * xs / ns
    us = (mxq(ts, 1, "e4m3") @ mxq(f64(W)[1:, 1:], 1, "e4m3").T) + f64(b)[1:]
    n = np.maximum(np.sqrt(np.sum(us * us, axis=1, keepdims=True)), EPS)
    nc = np.minimum(n, MAX_TAN_NORM)
    usc = us * (nc / n)
    return np.concatenate([cosh(nc), sinh(nc) * usc / nc], axis=1)

@@ -1,0 +1,392 @@
+from contextlib import ExitStack
+
+import concourse.mybir as mybir
+from concourse.masks import make_identity
+
+FLOPS = 2 * 1024 * 4096 * 1024
+
+F32 = mybir.dt.float32
+BF16 = mybir.dt.bfloat16
+U32 = mybir.dt.uint32
+U8 = mybir.dt.uint8
+FP8X4 = mybir.dt.float8_e4m3fn_x4
+ALU = mybir.AluOpType
+ACT = mybir.ActivationFunctionType
+AX = mybir.AxisListType
+
+P = 128
+NT = 8
+NCH = 8
+PAD = 32
+XP = PAD + 1024
+WP = XP // 2
+OPAD = 8
+WBUFS = 4
+X_LAG = 2
+
+
+def tile_lorentzmlp_pa_kernel(tc, x_hyp, W, b, out):
+    nc = tc.nc
+    with ExitStack() as ctx:
+        ctx.enter_context(tc.manual_schedule())
+        const = ctx.enter_context(tc.tile_pool(name="const", bufs=1))
+        wpool = ctx.enter_context(tc.tile_pool(name="wraw", bufs=WBUFS))
+        gpool = ctx.enter_context(tc.tile_pool(name="grouped", bufs=2))
+        tpool = ctx.enter_context(tc.tile_pool(name="ts", bufs=4))
+        spool = ctx.enter_context(tc.tile_pool(name="scratch", bufs=2))
+        opool = ctx.enter_context(tc.tile_pool(name="outs", bufs=4))
+        small = ctx.enter_context(tc.tile_pool(name="small", bufs=3))
+        psum = ctx.enter_context(tc.psum_pool(name="psum", bufs=8))
+
+        xraw = const.tile([P, NT * XP], BF16, align_bytes=64)
+        xr3 = xraw[:].rearrange("p (m c) -> p m c", c=XP)
+        xsrc = x_hyp.rearrange("(m p) c -> p m c", p=P)
+        wsrc = W[1:4097, :].rearrange("(c t p) k -> c p t k", t=4, p=P)
+        xq = const.tile([P, NT * 256], U32, align_bytes=64)
+        xsc = const.tile([P, NT * 256], U8, align_bytes=64)
+        wq = const.tile([P, NCH * 1024], U32, align_bytes=64)
+        wsc = const.tile([P, NCH * 1024], U8, align_bytes=64)
+        bias = const.tile([P, 4096], BF16)
+        ident_f = const.tile([P, P], F32)
+        ident_b = const.tile([P, P], BF16)
+        one = const.tile([P, 1], F32)
+        ex2 = const.tile([P, 2], F32)
+        warm = const.tile([P, 2], F32)
+        pw = const.tile([P, 16], F32)
+        pw3 = pw[:].rearrange("p (a i) -> p a i", i=8)
+        pc = const.tile([P, 16], F32)
+        v = const.tile([P, 8], F32)
+        v3 = v[:].rearrange("p (a i) -> p a i", a=2)
+        vp1 = const.tile([P, 8], F32)
+        po = const.tile([P, 16], F32)
+        rns = const.tile([P, 8], F32)
+        warg = const.tile([P, 8], F32)
+        dist = const.tile([P, 8], F32)
+        sx = const.tile([P, 8], F32)
+
+        wraw_t = {}
+        wbank = {}
+        wg_t = {}
+        ts_t = {}
+        xbank = {}
+        xg_t = {}
+
+        def load_w(c):
+            wraw = wpool.tile([P, 4 * XP], BF16, align_bytes=64, name="wraw")
+            nc.sync.dma_start(
+                out=wraw[:].rearrange("p (t k) -> p t k", k=XP)[:, :, PAD - 1 : XP],
+                in_=wsrc[c],
+            )
+            wraw_t[c] = wraw
+
+        def row_norm(m):
+            xs = xr3[:, m, PAD:XP]
+            if m % 2 == 0:
+                junk = spool.tile([P, 1024], BF16, name="junk")
+                nc.scalar.activation(
+                    out=junk[:], in_=xs, func=ACT.Square,
+                    accum_out=pw3[:, 0, m // 2 : m // 2 + 1],
+                )
+            else:
+                junkv = spool.tile([P, 1024], F32, name="junkv")
+                nc.vector.scalar_tensor_tensor(
+                    out=junkv[:], in0=xs, scalar=1.0, in1=xs,
+                    op0=ALU.mult, op1=ALU.mult,
+                    accum_out=pw3[:, 1, m // 2 : m // 2 + 1],
+                )
+
+        def scale_x(m):
+            j = 4 * (m % 2) + m // 2
+            ts = tpool.tile([P, 1024], BF16, align_bytes=64, name="ts")
+            nc.vector.tensor_scalar(
+                out=ts[:], in0=xr3[:, m, PAD:XP], scalar1=sx[:, j : j + 1],
+                scalar2=None, op0=ALU.mult,
+            )
+            ts_t[m] = ts
+
+        def transpose_x(m):
+            xt = psum.tile([P, 1024], BF16, tag="bank", name="xt")
+            ts4 = ts_t[m][:].rearrange("p (q t) -> p t q", t=4)
+            for g in range(2):
+                for t in range(4):
+                    col = (g * 4 + t) * P
+                    nc.tensor.transpose(
+                        xt[:, col : col + P], ts4[:, t, P * g : P * (g + 1)], ident_b[:]
+                    )
+            xbank[m] = xt
+
+        def regroup_x(m):
+            xg = gpool.tile([P, 1024], BF16, align_bytes=64, name="xg")
+            dst = xg[:].rearrange("p (g r t) -> p g r t", g=2, t=4)
+            src = xbank[m][:].rearrange("p (g t r) -> p g r t", g=2, t=4)
+            if m % 2 == 1 and m >= NT // 2:
+                nc.scalar.copy(out=dst, in_=src)
+            else:
+                nc.vector.tensor_copy(out=dst, in_=src)
+            xg_t[m] = xg
+
+        def quantise_x(m):
+            nc.vector.quantize_mx(
+                out=xq[:, m * 256 : (m + 1) * 256].bitcast(FP8X4),
+                scales=xsc[:, m * 256 : (m + 1) * 256],
+                in_=xg_t[m][:],
+            )
+
+        def transpose_w(c):
+            wf = wraw_t[c][:].bitcast(F32)
+            for g in range(2):
+                for tp in range(2):
+                    wt = psum.tile([P, 512], F32, tag="bank", name="wt")
+                    for tl in range(2):
+                        for u in range(2):
+                            col = (tl * 2 + u) * P
+                            src = (2 * tp + tl) * WP + PAD // 2 + 256 * g
+                            nc.tensor.transpose(
+                                wt[:, col : col + P],
+                                wf[:, src + u : src + 256 : 2],
+                                ident_f[:],
+                            )
+                    wbank[(c, 2 * g + tp)] = wt
+
+        def copy_w(c, k, on_vector):
+            if c not in wg_t:
+                wg = gpool.tile([P, 4096], BF16, align_bytes=64, name="wg")
+                wg_t[c] = wg
+            wgf = wg_t[c][:].bitcast(F32)
+            dst = wgf[:, k * 512 : (k + 1) * 512].rearrange(
+                "p (tl n u) -> p tl n u", tl=2, u=2
+            )
+            src = wbank[(c, k)][:].rearrange("p (tl u n) -> p tl n u", tl=2, u=2)
+            if on_vector:
+                nc.vector.tensor_copy(out=dst, in_=src)
+            else:
+                nc.scalar.copy(out=dst, in_=src)
+
+        def quantise_w(c):
+            nc.vector.quantize_mx(
+                out=wq[:, c * 1024 : (c + 1) * 1024].bitcast(FP8X4),
+                scales=wsc[:, c * 1024 : (c + 1) * 1024],
+                in_=wg_t[c][:],
+            )
+
+        for h in range(4):
+            nc.sync.dma_start(
+                out=xr3[:, 2 * h : 2 * h + 2, PAD - 1 : XP],
+                in_=xsrc[:, 2 * h : 2 * h + 2, :],
+            )
+        for c in range(WBUFS):
+            load_w(c)
+        make_identity(nc, ident_f[:])
+        make_identity(nc, ident_b[:])
+        nc.vector.memset(one[:], 1.0)
+        nc.vector.memset(ex2[:, 0:1], 0.5)
+        nc.vector.memset(ex2[:, 1:2], -0.5)
+        nc.scalar.activation(out=warm[:, 0:1], in_=one[:], func=ACT.Sqrt)
+        for m in range(NT - 1):
+            row_norm(m)
+        nc.vector.tensor_scalar_max(
+            out=v3, in0=xr3[:, :, PAD - 1].rearrange("p (i a) -> p a i", a=2),
+            scalar1=1.0 + 1e-7,
+        )
+        nc.vector.tensor_scalar_add(out=vp1[:], in0=v[:], scalar1=1.0)
+        nc.vector.scalar_tensor_tensor(
+            out=pc[:, 8:16], in0=v[:], scalar=-1.0, in1=vp1[:],
+            op0=ALU.add, op1=ALU.mult,
+        )
+        row_norm(NT - 1)
+        nc.vector.tensor_scalar_max(
+            out=pc[:, 0:8].rearrange("p (a i) -> p a i", a=2), in0=pw3[:, :, 0:4],
+            scalar1=1e-14,
+        )
+        nc.scalar.activation(out=po[:], in_=pc[:], func=ACT.Sqrt)
+        nc.vector.tensor_tensor(out=warg[:], in0=v[:], in1=po[:, 8:16], op=ALU.add)
+        nc.vector.reciprocal(out=rns[:], in_=po[:, 0:8])
+        nc.scalar.activation(out=dist[:], in_=warg[:], func=ACT.Ln)
+        nc.vector.tensor_tensor(out=sx[:], in0=rns[:], in1=dist[:], op=ALU.mult)
+
+        for c in range(NCH + X_LAG):
+            if c < NCH:
+                transpose_w(c)
+            if 1 <= c <= NT:
+                transpose_x(c - 1)
+            if c + WBUFS < NCH:
+                load_w(c + WBUFS)
+            if c == NCH - 1:
+                for h in range(2):
+                    nc.sync.dma_start(
+                        out=bias[:, 2048 * h : 2048 * (h + 1)],
+                        in_=b[1 + 2048 * h : 1 + 2048 * (h + 1)].partition_broadcast(P),
+                    )
+            if c == 0:
+                scale_x(0)
+                scale_x(1)
+            if c < NCH:
+                for k in range(4):
+                    copy_w(c, k, False)
+            m = c - X_LAG
+            if c == NCH:
+                quantise_w(c - 1)
+            if 0 <= m:
+                regroup_x(m)
+            if 1 <= c < NCH:
+                quantise_w(c - 1)
+            if c + 2 < NT:
+                scale_x(c + 2)
+            if 0 <= m and not (m % 2 == 1 and m >= NT // 2):
+                quantise_x(m)
+            if m % 2 == 0 and m - 1 >= NT // 2:
+                quantise_x(m - 1)
+        nc.scalar.activation(out=warm[:, 1:2], in_=one[:], func=ACT.Exp)
+
+        ot_t = {}
+        acc_t = {}
+        n2_t = {}
+        nr_t = {}
+        ncl_t = {}
+        ep_t = {}
+        em_t = {}
+        sc_t = {}
+
+        def columns(m, lo, hi):
+            return ot_t[m][:, OPAD + lo : OPAD + hi]
+
+        def scale_on_gpsimd(m, lo, hi):
+            seg = columns(m, lo, hi)
+            nc.gpsimd.tensor_scalar(
+                out=seg, in0=seg, scalar1=sc_t[m][:, 0:1], scalar2=0.0,
+                op0=ALU.mult, op1=ALU.add,
+            )
+
+        def scale_on_vector(m, lo, hi):
+            seg = columns(m, lo, hi)
+            nc.vector.tensor_scalar(
+                out=seg, in0=seg, scalar1=sc_t[m][:, 0:1], scalar2=None, op0=ALU.mult
+            )
+
+        def scale_on_scalar(m, lo, hi):
+            seg = columns(m, lo, hi)
+            nc.scalar.activation(out=seg, in_=seg, func=ACT.Copy, scale=sc_t[m][:, 0:1])
+
+        def store(m, lo, hi):
+            nc.sync.dma_start(
+                out=out[m * P : (m + 1) * P, lo:hi],
+                in_=ot_t[m][:, OPAD - 1 + lo : OPAD - 1 + hi],
+            )
+
+        def norm_sum(m):
+            n2 = small.tile([P, 1], F32, name="n2")
+            junk8 = small.tile([P, 8], F32, name="junk8")
+            width = acc_t[m][:].shape[1]
+            nc.scalar.activation(
+                out=junk8[:, 0:width], in_=acc_t[m][:], func=ACT.Copy, accum_out=n2[:]
+            )
+            n2_t[m] = n2
+
+        def norm_root(m):
+            pr = small.tile([P, 2], F32, name="pr")
+            nc.gpsimd.tensor_scalar(
+                out=pr[:], in0=n2_t[m][:].to_broadcast([P, 2]), scalar1=1e-14,
+                scalar2=None, op0=ALU.max,
+            )
+            nr = small.tile([P, 2], F32, name="nr")
+            nc.gpsimd.tensor_tensor(out=nr[:], in0=pr[:], in1=ex2[:], op=ALU.pow)
+            ncl = small.tile([P, 1], F32, name="ncl")
+            nc.gpsimd.tensor_scalar(
+                out=ncl[:], in0=nr[:, 0:1], scalar1=10.0, scalar2=None, op0=ALU.min
+            )
+            nr_t[m] = nr
+            ncl_t[m] = ncl
+
+        def norm_exp(m):
+            ep = small.tile([P, 1], F32, name="ep")
+            nc.scalar.activation(out=ep[:], in_=ncl_t[m][:], func=ACT.Exp)
+            em = small.tile([P, 1], F32, name="em")
+            nc.scalar.activation(out=em[:], in_=ncl_t[m][:], func=ACT.Exp, scale=-1.0)
+            ep_t[m] = ep
+            em_t[m] = em
+
+        def norm_end(m):
+            sh = small.tile([P, 1], F32, name="sh")
+            nc.vector.tensor_scalar(
+                out=sh[:], in0=ep_t[m][:], scalar1=em_t[m][:, 0:1], scalar2=0.5,
+                op0=ALU.subtract, op1=ALU.mult,
+            )
+            sc = small.tile([P, 1], F32, name="sc")
+            nc.vector.tensor_scalar(
+                out=sc[:], in0=sh[:], scalar1=nr_t[m][:, 1:2], scalar2=None, op0=ALU.mult
+            )
+            nc.vector.tensor_scalar(
+                out=ot_t[m][:, OPAD - 1 : OPAD], in0=ep_t[m][:],
+                scalar1=em_t[m][:, 0:1], scalar2=0.5, op0=ALU.add, op1=ALU.mult,
+            )
+            sc_t[m] = sc
+
+        for m in range(NT):
+            last = m == NT - 1
+            hw = 1 if last else 2
+            ot = opool.tile([P, OPAD + 4096], F32, name="ot")
+            ot_t[m] = ot
+            acc = small.tile([P, NCH // hw], F32, name="acc8" if last else "acc")
+            acc_t[m] = acc
+            for c in range(NCH):
+                ps = psum.tile([P, 512], F32, tag="bank", name="ps")
+                for g in range(2):
+                    lo = (2 * m + g) * P
+                    ro = c * 1024 + g * 512
+                    nc.tensor.matmul_mx(
+                        out=ps[:],
+                        lhsT=xq[:, lo : lo + P].bitcast(FP8X4),
+                        lhsT_scale=xsc[:, lo : lo + P],
+                        rhs=wq[:, ro : ro + 512].bitcast(FP8X4),
+                        rhs_scale=wsc[:, ro : ro + 512],
+                        start=(g == 0),
+                        stop=(g == 1),
+                    )
+                nc.vector.tensor_tensor(
+                    out=ot[:, OPAD + 512 * c : OPAD + 512 * (c + 1)], in0=ps[:],
+                    in1=bias[:, 512 * c : 512 * (c + 1)], op=ALU.add,
+                )
+                if (c + 1) % hw == 0:
+                    h = c // hw
+                    junk = spool.tile([P, 1024], BF16, name="junk")
+                    nc.scalar.activation(
+                        out=junk[:, 0 : 512 * hw],
+                        in_=ot[:, OPAD + 512 * hw * h : OPAD + 512 * hw * (h + 1)],
+                        func=ACT.Square, accum_out=acc[:, h : h + 1],
+                    )
+                if m == 0 and c == 3:
+                    quantise_x(NT - 1)
+                if m > 0 and c == 1:
+                    norm_root(m - 1)
+                    if m > 1:
+                        scale_on_gpsimd(m - 2, 3072, 4096)
+                        store(m - 2, 2049, 4097)
+                if m > 0 and c == 3:
+                    norm_exp(m - 1)
+                if c == NCH - 1:
+                    norm_sum(m)
+                    if m > 0:
+                        norm_end(m - 1)
+                        scale_on_vector(m - 1, 0, 1536)
+                        if not last:
+                            scale_on_gpsimd(m - 1, 1536, 2048)
+                            store(m - 1, 0, 2049)
+                            scale_on_gpsimd(m - 1, 2048, 3072)
+
+        m = NT - 1
+        norm_root(m)
+        scale_on_vector(m - 1, 1536, 2048)
+        store(m - 1, 0, 2049)
+        scale_on_scalar(m - 1, 2048, 3072)
+        scale_on_vector(m - 1, 3072, 4096)
+        store(m - 1, 2049, 4097)
+        norm_exp(m)
+        norm_end(m)
+        scale_on_vector(m, 0, 1024)
+        store(m, 0, 1025)
+        scale_on_gpsimd(m, 1024, 2048)
+        store(m, 1025, 2049)
+        scale_on_scalar(m, 2048, 3072)
+        store(m, 2049, 3073)
+        scale_on_vector(m, 3072, 4096)
+        store(m, 3073, 4097)

@@ -12,7 +12,6 @@ U8 = mybir.dt.uint8
 FP8X4 = mybir.dt.float8_e4m3fn_x4
 ALU = mybir.AluOpType
 ACT = mybir.ActivationFunctionType
-AX = mybir.AxisListType
 
 P = 128
 NT = 8
@@ -22,7 +21,7 @@ XP = PAD + 1024
 WP = XP // 2
 OPAD = 8
 WBUFS = 4
-X_LAG = 2
+GT = 4
 
 
 def tile_lorentzmlp_pa_kernel(tc, x_hyp, W, b, out):
@@ -32,7 +31,7 @@ def tile_lorentzmlp_pa_kernel(tc, x_hyp, W, b, out):
         const = ctx.enter_context(tc.tile_pool(name="const", bufs=1))
         wpool = ctx.enter_context(tc.tile_pool(name="wraw", bufs=WBUFS))
         gpool = ctx.enter_context(tc.tile_pool(name="grouped", bufs=2))
-        tpool = ctx.enter_context(tc.tile_pool(name="ts", bufs=4))
+        tpool = ctx.enter_context(tc.tile_pool(name="ts", bufs=8))
         spool = ctx.enter_context(tc.tile_pool(name="scratch", bufs=2))
         opool = ctx.enter_context(tc.tile_pool(name="outs", bufs=4))
         small = ctx.enter_context(tc.tile_pool(name="small", bufs=3))
@@ -48,21 +47,18 @@ def tile_lorentzmlp_pa_kernel(tc, x_hyp, W, b, out):
         wsc = const.tile([P, NCH * 1024], U8, align_bytes=64)
         bias = const.tile([P, 4096], BF16)
         ident_f = const.tile([P, P], F32)
-        ident_b = const.tile([P, P], BF16)
         one = const.tile([P, 1], F32)
-        ex2 = const.tile([P, 2], F32)
+        half = const.tile([P, 8], F32)
         warm = const.tile([P, 2], F32)
-        pw = const.tile([P, 16], F32)
-        pw3 = pw[:].rearrange("p (a i) -> p a i", i=8)
-        pc = const.tile([P, 16], F32)
-        v = const.tile([P, 8], F32)
-        v3 = v[:].rearrange("p (a i) -> p a i", a=2)
-        vp1 = const.tile([P, 8], F32)
-        po = const.tile([P, 16], F32)
-        rns = const.tile([P, 8], F32)
-        warg = const.tile([P, 8], F32)
-        dist = const.tile([P, 8], F32)
-        sx = const.tile([P, 8], F32)
+        ss = const.tile([P, NT], F32)
+        v = const.tile([P, NT], F32)
+        vm1 = const.tile([P, NT], F32)
+        vp1 = const.tile([P, NT], F32)
+        radicand = const.tile([P, 2 * NT], F32)
+        root = const.tile([P, 2 * NT], F32)
+        warg = const.tile([P, NT], F32)
+        dist = const.tile([P, NT], F32)
+        sx = const.tile([P, NT], F32)
 
         wraw_t = {}
         wbank = {}
@@ -73,56 +69,99 @@ def tile_lorentzmlp_pa_kernel(tc, x_hyp, W, b, out):
 
         def load_w(c):
             wraw = wpool.tile([P, 4 * XP], BF16, align_bytes=64, name="wraw")
-            nc.sync.dma_start(
-                out=wraw[:].rearrange("p (t k) -> p t k", k=XP)[:, :, PAD - 1 : XP],
-                in_=wsrc[c],
-            )
+            dst = wraw[:].rearrange("p (t k) -> p t k", k=XP)
+            for tp in range(2):
+                nc.sync.dma_start(
+                    out=dst[:, 2 * tp : 2 * tp + 2, PAD - 1 : XP],
+                    in_=wsrc[c][:, 2 * tp : 2 * tp + 2, :],
+                )
             wraw_t[c] = wraw
+
+        def load_x(h):
+            for m in range(GT * h, GT * (h + 1), 2):
+                nc.sync.dma_start(
+                    out=xr3[:, m : m + 2, PAD - 1 : XP], in_=xsrc[:, m : m + 2, :]
+                )
+
+        def load_bias(h):
+            nc.sync.dma_start(
+                out=bias[:, 2048 * h : 2048 * (h + 1)],
+                in_=b[1 + 2048 * h : 1 + 2048 * (h + 1)].partition_broadcast(P),
+            )
 
         def row_norm(m):
             xs = xr3[:, m, PAD:XP]
             if m % 2 == 0:
                 junk = spool.tile([P, 1024], BF16, name="junk")
                 nc.scalar.activation(
-                    out=junk[:], in_=xs, func=ACT.Square,
-                    accum_out=pw3[:, 0, m // 2 : m // 2 + 1],
+                    out=junk[:], in_=xs, func=ACT.Square, accum_out=ss[:, m : m + 1]
                 )
             else:
                 junkv = spool.tile([P, 1024], F32, name="junkv")
                 nc.vector.scalar_tensor_tensor(
                     out=junkv[:], in0=xs, scalar=1.0, in1=xs,
-                    op0=ALU.mult, op1=ALU.mult,
-                    accum_out=pw3[:, 1, m // 2 : m // 2 + 1],
+                    op0=ALU.mult, op1=ALU.mult, accum_out=ss[:, m : m + 1],
                 )
 
+        def log_map(h):
+            lo, hi = GT * h, GT * (h + 1)
+            a, r = 2 * GT * h, 2 * GT * h + GT
+            nc.gpsimd.tensor_scalar(
+                out=v[:, lo:hi], in0=xr3[:, lo:hi, PAD - 1], scalar1=1.0 + 1e-7,
+                scalar2=None, op0=ALU.max,
+            )
+            nc.gpsimd.tensor_scalar(
+                out=vm1[:, lo:hi], in0=v[:, lo:hi], scalar1=-1.0, scalar2=None, op0=ALU.add
+            )
+            nc.gpsimd.tensor_scalar(
+                out=vp1[:, lo:hi], in0=v[:, lo:hi], scalar1=1.0, scalar2=None, op0=ALU.add
+            )
+            nc.gpsimd.tensor_tensor(
+                out=radicand[:, r : r + GT], in0=vm1[:, lo:hi], in1=vp1[:, lo:hi], op=ALU.mult
+            )
+            nc.gpsimd.tensor_scalar(
+                out=radicand[:, a : a + GT], in0=ss[:, lo:hi], scalar1=1e-14,
+                scalar2=None, op0=ALU.max,
+            )
+            nc.gpsimd.tensor_tensor(
+                out=root[:, a : a + 2 * GT], in0=radicand[:, a : a + 2 * GT],
+                in1=half[:], op=ALU.pow,
+            )
+            nc.gpsimd.tensor_tensor(
+                out=warg[:, lo:hi], in0=v[:, lo:hi], in1=root[:, r : r + GT], op=ALU.add
+            )
+            nc.scalar.activation(out=dist[:, lo:hi], in_=warg[:, lo:hi], func=ACT.Ln)
+            nc.gpsimd.tensor_tensor(
+                out=sx[:, lo:hi], in0=root[:, a : a + GT], in1=dist[:, lo:hi], op=ALU.mult
+            )
+
         def scale_x(m):
-            j = 4 * (m % 2) + m // 2
             ts = tpool.tile([P, 1024], BF16, align_bytes=64, name="ts")
             nc.vector.tensor_scalar(
-                out=ts[:], in0=xr3[:, m, PAD:XP], scalar1=sx[:, j : j + 1],
+                out=ts[:], in0=xr3[:, m, PAD:XP], scalar1=sx[:, m : m + 1],
                 scalar2=None, op0=ALU.mult,
             )
             ts_t[m] = ts
 
         def transpose_x(m):
-            xt = psum.tile([P, 1024], BF16, tag="bank", name="xt")
-            ts4 = ts_t[m][:].rearrange("p (q t) -> p t q", t=4)
+            xt = psum.tile([P, 512], F32, tag="bank", name="xt")
+            words = ts_t[m][:].bitcast(F32)
             for g in range(2):
-                for t in range(4):
-                    col = (g * 4 + t) * P
+                for u in range(2):
+                    col = (g * 2 + u) * P
                     nc.tensor.transpose(
-                        xt[:, col : col + P], ts4[:, t, P * g : P * (g + 1)], ident_b[:]
+                        xt[:, col : col + P],
+                        words[:, 256 * g + u : 256 * (g + 1) : 2],
+                        ident_f[:],
                     )
             xbank[m] = xt
 
         def regroup_x(m):
             xg = gpool.tile([P, 1024], BF16, align_bytes=64, name="xg")
-            dst = xg[:].rearrange("p (g r t) -> p g r t", g=2, t=4)
-            src = xbank[m][:].rearrange("p (g t r) -> p g r t", g=2, t=4)
-            if m % 2 == 1 and m >= NT // 2:
-                nc.scalar.copy(out=dst, in_=src)
-            else:
-                nc.vector.tensor_copy(out=dst, in_=src)
+            nc.vector.tensor_copy(
+                out=xg[:].bitcast(F32).rearrange("p (g r u) -> p g r u", g=2, u=2),
+                in_=xbank[m][:].rearrange("p (g u r) -> p g r u", g=2, u=2),
+            )
             xg_t[m] = xg
 
         def quantise_x(m):
@@ -134,8 +173,8 @@ def tile_lorentzmlp_pa_kernel(tc, x_hyp, W, b, out):
 
         def transpose_w(c):
             wf = wraw_t[c][:].bitcast(F32)
-            for g in range(2):
-                for tp in range(2):
+            for tp in range(2):
+                for g in range(2):
                     wt = psum.tile([P, 512], F32, tag="bank", name="wt")
                     for tl in range(2):
                         for u in range(2):
@@ -148,19 +187,17 @@ def tile_lorentzmlp_pa_kernel(tc, x_hyp, W, b, out):
                             )
                     wbank[(c, 2 * g + tp)] = wt
 
-        def copy_w(c, k, on_vector):
-            if c not in wg_t:
-                wg = gpool.tile([P, 4096], BF16, align_bytes=64, name="wg")
-                wg_t[c] = wg
-            wgf = wg_t[c][:].bitcast(F32)
-            dst = wgf[:, k * 512 : (k + 1) * 512].rearrange(
-                "p (tl n u) -> p tl n u", tl=2, u=2
-            )
-            src = wbank[(c, k)][:].rearrange("p (tl u n) -> p tl n u", tl=2, u=2)
-            if on_vector:
-                nc.vector.tensor_copy(out=dst, in_=src)
-            else:
-                nc.scalar.copy(out=dst, in_=src)
+        def copy_w(c):
+            wg = gpool.tile([P, 4096], BF16, align_bytes=64, name="wg")
+            wg_t[c] = wg
+            wgf = wg[:].bitcast(F32)
+            for k in (0, 2, 1, 3):
+                nc.scalar.copy(
+                    out=wgf[:, k * 512 : (k + 1) * 512].rearrange(
+                        "p (tl n u) -> p tl n u", tl=2, u=2
+                    ),
+                    in_=wbank[(c, k)][:].rearrange("p (tl u n) -> p tl n u", tl=2, u=2),
+                )
 
         def quantise_w(c):
             nc.vector.quantize_mx(
@@ -169,77 +206,45 @@ def tile_lorentzmlp_pa_kernel(tc, x_hyp, W, b, out):
                 in_=wg_t[c][:],
             )
 
-        for h in range(4):
-            nc.sync.dma_start(
-                out=xr3[:, 2 * h : 2 * h + 2, PAD - 1 : XP],
-                in_=xsrc[:, 2 * h : 2 * h + 2, :],
-            )
-        for c in range(WBUFS):
-            load_w(c)
-        make_identity(nc, ident_f[:])
-        make_identity(nc, ident_b[:])
-        nc.vector.memset(one[:], 1.0)
-        nc.vector.memset(ex2[:, 0:1], 0.5)
-        nc.vector.memset(ex2[:, 1:2], -0.5)
-        nc.scalar.activation(out=warm[:, 0:1], in_=one[:], func=ACT.Sqrt)
-        for m in range(NT - 1):
-            row_norm(m)
-        nc.vector.tensor_scalar_max(
-            out=v3, in0=xr3[:, :, PAD - 1].rearrange("p (i a) -> p a i", a=2),
-            scalar1=1.0 + 1e-7,
-        )
-        nc.vector.tensor_scalar_add(out=vp1[:], in0=v[:], scalar1=1.0)
-        nc.vector.scalar_tensor_tensor(
-            out=pc[:, 8:16], in0=v[:], scalar=-1.0, in1=vp1[:],
-            op0=ALU.add, op1=ALU.mult,
-        )
-        row_norm(NT - 1)
-        nc.vector.tensor_scalar_max(
-            out=pc[:, 0:8].rearrange("p (a i) -> p a i", a=2), in0=pw3[:, :, 0:4],
-            scalar1=1e-14,
-        )
-        nc.scalar.activation(out=po[:], in_=pc[:], func=ACT.Sqrt)
-        nc.vector.tensor_tensor(out=warg[:], in0=v[:], in1=po[:, 8:16], op=ALU.add)
-        nc.vector.reciprocal(out=rns[:], in_=po[:, 0:8])
-        nc.scalar.activation(out=dist[:], in_=warg[:], func=ACT.Ln)
-        nc.vector.tensor_tensor(out=sx[:], in0=rns[:], in1=dist[:], op=ALU.mult)
-
-        for c in range(NCH + X_LAG):
-            if c < NCH:
-                transpose_w(c)
-            if 1 <= c <= NT:
-                transpose_x(c - 1)
-            if c + WBUFS < NCH:
-                load_w(c + WBUFS)
-            if c == NCH - 1:
-                for h in range(2):
-                    nc.sync.dma_start(
-                        out=bias[:, 2048 * h : 2048 * (h + 1)],
-                        in_=b[1 + 2048 * h : 1 + 2048 * (h + 1)].partition_broadcast(P),
-                    )
-            if c == 0:
-                scale_x(0)
-                scale_x(1)
-            if c < NCH:
-                for k in range(4):
-                    copy_w(c, k, False)
-            m = c - X_LAG
-            if c == NCH:
-                quantise_w(c - 1)
-            if 0 <= m:
-                regroup_x(m)
-            if 1 <= c < NCH:
-                quantise_w(c - 1)
-            if c + 2 < NT:
-                scale_x(c + 2)
-            if 0 <= m and not (m % 2 == 1 and m >= NT // 2):
-                quantise_x(m)
-            if m % 2 == 0 and m - 1 >= NT // 2:
-                quantise_x(m - 1)
-        nc.scalar.activation(out=warm[:, 1:2], in_=one[:], func=ACT.Exp)
-
         ot_t = {}
         acc_t = {}
+        ps_t = {}
+
+        def multiply(m, c):
+            ps = psum.tile([P, 512], F32, tag="bank", name="ps")
+            for g in range(2):
+                lo = (2 * m + g) * P
+                ro = c * 1024 + g * 512
+                nc.tensor.matmul_mx(
+                    out=ps[:],
+                    lhsT=xq[:, lo : lo + P].bitcast(FP8X4),
+                    lhsT_scale=xsc[:, lo : lo + P],
+                    rhs=wq[:, ro : ro + 512].bitcast(FP8X4),
+                    rhs_scale=wsc[:, ro : ro + 512],
+                    start=(g == 0),
+                    stop=(g == 1),
+                )
+            ps_t[(m, c)] = ps
+
+        def evict(m, c):
+            if m not in ot_t:
+                ot = opool.tile([P, OPAD + 4096], F32, name="ot")
+                ot_t[m] = ot
+            nc.vector.tensor_tensor(
+                out=columns(m, 512 * c, 512 * (c + 1)), in0=ps_t[(m, c)][:],
+                in1=bias[:, 512 * c : 512 * (c + 1)], op=ALU.add,
+            )
+
+        def square(m, lo, hi, j):
+            if m not in acc_t:
+                acc = small.tile([P, 8], F32, name="acc")
+                acc_t[m] = acc
+            junk = spool.tile([P, 1024], BF16, name="junk")
+            nc.scalar.activation(
+                out=junk[:, 0 : hi - lo], in_=columns(m, lo, hi),
+                func=ACT.Square, accum_out=acc_t[m][:, j : j + 1],
+            )
+
         n2_t = {}
         nr_t = {}
         ncl_t = {}
@@ -273,12 +278,12 @@ def tile_lorentzmlp_pa_kernel(tc, x_hyp, W, b, out):
                 in_=ot_t[m][:, OPAD - 1 + lo : OPAD - 1 + hi],
             )
 
-        def norm_sum(m):
+        def norm_sum(m, parts):
             n2 = small.tile([P, 1], F32, name="n2")
             junk8 = small.tile([P, 8], F32, name="junk8")
-            width = acc_t[m][:].shape[1]
             nc.scalar.activation(
-                out=junk8[:, 0:width], in_=acc_t[m][:], func=ACT.Copy, accum_out=n2[:]
+                out=junk8[:, 0:parts], in_=acc_t[m][:, 0:parts], func=ACT.Copy,
+                accum_out=n2[:],
             )
             n2_t[m] = n2
 
@@ -289,10 +294,12 @@ def tile_lorentzmlp_pa_kernel(tc, x_hyp, W, b, out):
                 scalar2=None, op0=ALU.max,
             )
             nr = small.tile([P, 2], F32, name="nr")
-            nc.gpsimd.tensor_tensor(out=nr[:], in0=pr[:], in1=ex2[:], op=ALU.pow)
+            nc.gpsimd.tensor_tensor(
+                out=nr[:], in0=pr[:], in1=half[:, GT - 1 : GT + 1], op=ALU.pow
+            )
             ncl = small.tile([P, 1], F32, name="ncl")
             nc.gpsimd.tensor_scalar(
-                out=ncl[:], in0=nr[:, 0:1], scalar1=10.0, scalar2=None, op0=ALU.min
+                out=ncl[:], in0=nr[:, 1:2], scalar1=10.0, scalar2=None, op0=ALU.min
             )
             nr_t[m] = nr
             ncl_t[m] = ncl
@@ -311,80 +318,96 @@ def tile_lorentzmlp_pa_kernel(tc, x_hyp, W, b, out):
                 out=sh[:], in0=ep_t[m][:], scalar1=em_t[m][:, 0:1], scalar2=0.5,
                 op0=ALU.subtract, op1=ALU.mult,
             )
-            sc = small.tile([P, 1], F32, name="sc")
-            nc.vector.tensor_scalar(
-                out=sc[:], in0=sh[:], scalar1=nr_t[m][:, 1:2], scalar2=None, op0=ALU.mult
-            )
             nc.vector.tensor_scalar(
                 out=ot_t[m][:, OPAD - 1 : OPAD], in0=ep_t[m][:],
                 scalar1=em_t[m][:, 0:1], scalar2=0.5, op0=ALU.add, op1=ALU.mult,
             )
+            sc = small.tile([P, 1], F32, name="sc")
+            nc.vector.tensor_scalar(
+                out=sc[:], in0=sh[:], scalar1=nr_t[m][:, 0:1], scalar2=None, op0=ALU.mult
+            )
             sc_t[m] = sc
 
-        for m in range(NT):
-            last = m == NT - 1
-            hw = 1 if last else 2
-            ot = opool.tile([P, OPAD + 4096], F32, name="ot")
-            ot_t[m] = ot
-            acc = small.tile([P, NCH // hw], F32, name="acc8" if last else "acc")
-            acc_t[m] = acc
-            for c in range(NCH):
-                ps = psum.tile([P, 512], F32, tag="bank", name="ps")
-                for g in range(2):
-                    lo = (2 * m + g) * P
-                    ro = c * 1024 + g * 512
-                    nc.tensor.matmul_mx(
-                        out=ps[:],
-                        lhsT=xq[:, lo : lo + P].bitcast(FP8X4),
-                        lhsT_scale=xsc[:, lo : lo + P],
-                        rhs=wq[:, ro : ro + 512].bitcast(FP8X4),
-                        rhs_scale=wsc[:, ro : ro + 512],
-                        start=(g == 0),
-                        stop=(g == 1),
-                    )
-                nc.vector.tensor_tensor(
-                    out=ot[:, OPAD + 512 * c : OPAD + 512 * (c + 1)], in0=ps[:],
-                    in1=bias[:, 512 * c : 512 * (c + 1)], op=ALU.add,
-                )
-                if (c + 1) % hw == 0:
-                    h = c // hw
-                    junk = spool.tile([P, 1024], BF16, name="junk")
-                    nc.scalar.activation(
-                        out=junk[:, 0 : 512 * hw],
-                        in_=ot[:, OPAD + 512 * hw * h : OPAD + 512 * hw * (h + 1)],
-                        func=ACT.Square, accum_out=acc[:, h : h + 1],
-                    )
-                if m == 0 and c == 3:
-                    quantise_x(NT - 1)
-                if m > 0 and c == 1:
-                    norm_root(m - 1)
-                    if m > 1:
-                        scale_on_gpsimd(m - 2, 3072, 4096)
-                        store(m - 2, 2049, 4097)
-                if m > 0 and c == 3:
-                    norm_exp(m - 1)
-                if c == NCH - 1:
-                    norm_sum(m)
-                    if m > 0:
-                        norm_end(m - 1)
-                        scale_on_vector(m - 1, 0, 1536)
-                        if not last:
-                            scale_on_gpsimd(m - 1, 1536, 2048)
-                            store(m - 1, 0, 2049)
-                            scale_on_gpsimd(m - 1, 2048, 3072)
+        load_w(0)
+        load_x(0)
+        load_w(1)
+        load_x(1)
+        load_bias(0)
+        load_w(2)
+        load_w(3)
+        make_identity(nc, ident_f[:])
+        nc.vector.memset(one[:], 1.0)
+        nc.vector.memset(half[:, 0:GT], -0.5)
+        nc.vector.memset(half[:, GT : 2 * GT], 0.5)
+        nc.scalar.activation(out=warm[:, 0:1], in_=one[:], func=ACT.Ln)
 
-        m = NT - 1
-        norm_root(m)
-        scale_on_vector(m - 1, 1536, 2048)
-        store(m - 1, 0, 2049)
-        scale_on_scalar(m - 1, 2048, 3072)
+        for s in range(NCH):
+            transpose_w(s)
+            if 1 <= s <= 4:
+                transpose_x(2 * s - 2)
+                transpose_x(2 * s - 1)
+            if s + WBUFS < NCH:
+                load_w(s + WBUFS)
+            if s == 1:
+                load_bias(1)
+            copy_w(s)
+            for c in range(NCH):
+                if c == s - 2 and c >= 1 or c == 0 and s == 3:
+                    evict(0, c)
+                    if c % 2 == 1:
+                        square(0, 512 * (c - 1), 512 * (c + 1), c // 2)
+            if s <= 1:
+                for m in range(GT * s, GT * (s + 1)):
+                    row_norm(m)
+                log_map(s)
+            quantise_w(s)
+            if 1 <= s <= 4:
+                regroup_x(2 * s - 2)
+                regroup_x(2 * s - 1)
+                quantise_x(2 * s - 2)
+                quantise_x(2 * s - 1)
+            if s <= 1:
+                for m in range(GT * s, GT * (s + 1)):
+                    scale_x(m)
+            if s == 2:
+                nc.scalar.activation(out=warm[:, 1:2], in_=one[:], func=ACT.Exp)
+                multiply(0, 0)
+            if s >= 2:
+                multiply(0, s - 1)
+
+        order = [(1, 0), (1, 1), (0, 7)]
+        order += [(1, c) for c in range(2, NCH)]
+        order += [(m, c) for m in range(2, NT) for c in range(NCH)]
+        evict(0, 6)
+        last = NT - 1
+        for m, c in order:
+            multiply(m, c)
+            evict(m, c)
+            if m == last and c >= NCH - 2:
+                square(m, 512 * c, 512 * (c + 1), c - NCH + 5)
+            elif c % 2 == 1:
+                square(m, 512 * (c - 1), 512 * (c + 1), c // 2)
+            if c == NCH - 1:
+                norm_sum(m, 5 if m == last else 4)
+                norm_root(m)
+                norm_exp(m)
+                if 1 <= m < last:
+                    scale_on_gpsimd(m - 1, 3072, 4096)
+                    store(m - 1, 2049, 4097)
+            if m >= 1 and c == (4 if m == 1 else 3):
+                norm_end(m - 1)
+                scale_on_gpsimd(m - 1, 0, 1024)
+                scale_on_gpsimd(m - 1, 1024, 2048)
+                store(m - 1, 0, 2049)
+                scale_on_gpsimd(m - 1, 2048, 3072)
+
+        m = last
         scale_on_vector(m - 1, 3072, 4096)
         store(m - 1, 2049, 4097)
-        norm_exp(m)
         norm_end(m)
         scale_on_vector(m, 0, 1024)
         store(m, 0, 1025)
-        scale_on_gpsimd(m, 1024, 2048)
+        scale_on_vector(m, 1024, 2048)
         store(m, 1025, 2049)
         scale_on_scalar(m, 2048, 3072)
         store(m, 2049, 3073)

@@ -21,6 +21,13 @@ XP = PAD + 1024
 WP = XP // 2
 OPAD = 8
 WBUFS = 4
+NORM_S = (0, 2, 4)
+OB = 5
+XS = 2
+XSCHED = ((0, 1), (2, 3), (4, 5), (6, 7))
+ROOT, Q3, CLAMP, END = 1, 1, 3, 6
+GE = 3968
+LEND = 5
 GT = 4
 
 
@@ -31,9 +38,9 @@ def tile_lorentzmlp_pa_kernel(tc, x_hyp, W, b, out):
         const = ctx.enter_context(tc.tile_pool(name="const", bufs=1))
         wpool = ctx.enter_context(tc.tile_pool(name="wraw", bufs=WBUFS))
         gpool = ctx.enter_context(tc.tile_pool(name="grouped", bufs=2))
-        tpool = ctx.enter_context(tc.tile_pool(name="ts", bufs=8))
+        tpool = ctx.enter_context(tc.tile_pool(name="ts", bufs=4))
         spool = ctx.enter_context(tc.tile_pool(name="scratch", bufs=2))
-        opool = ctx.enter_context(tc.tile_pool(name="outs", bufs=4))
+        opool = ctx.enter_context(tc.tile_pool(name="outs", bufs=OB))
         small = ctx.enter_context(tc.tile_pool(name="small", bufs=3))
         psum = ctx.enter_context(tc.psum_pool(name="psum", bufs=8))
 
@@ -48,14 +55,15 @@ def tile_lorentzmlp_pa_kernel(tc, x_hyp, W, b, out):
         bias = const.tile([P, 4096], BF16)
         ident_f = const.tile([P, P], F32)
         one = const.tile([P, 1], F32)
-        half = const.tile([P, 8], F32)
+        mhalf = const.tile([P, 1], F32)
+        acc = const.tile([P, 6 * NT], F32)
         warm = const.tile([P, 2], F32)
         ss = const.tile([P, NT], F32)
         v = const.tile([P, NT], F32)
-        vm1 = const.tile([P, NT], F32)
         vp1 = const.tile([P, NT], F32)
         radicand = const.tile([P, 2 * NT], F32)
         root = const.tile([P, 2 * NT], F32)
+        rns = const.tile([P, NT], F32)
         warg = const.tile([P, NT], F32)
         dist = const.tile([P, NT], F32)
         sx = const.tile([P, NT], F32)
@@ -78,7 +86,7 @@ def tile_lorentzmlp_pa_kernel(tc, x_hyp, W, b, out):
             wraw_t[c] = wraw
 
         def load_x(h):
-            for m in range(GT * h, GT * (h + 1), 2):
+            for m in range(0, NT, 2):
                 nc.sync.dma_start(
                     out=xr3[:, m : m + 2, PAD - 1 : XP], in_=xsrc[:, m : m + 2, :]
                 )
@@ -91,49 +99,35 @@ def tile_lorentzmlp_pa_kernel(tc, x_hyp, W, b, out):
 
         def row_norm(m):
             xs = xr3[:, m, PAD:XP]
-            if m % 2 == 0:
+            if m in NORM_S:
                 junk = spool.tile([P, 1024], BF16, name="junk")
                 nc.scalar.activation(
                     out=junk[:], in_=xs, func=ACT.Square, accum_out=ss[:, m : m + 1]
                 )
             else:
-                junkv = spool.tile([P, 1024], F32, name="junkv")
+                junkv = spool.tile([P, 1024], BF16, name="junkv")
                 nc.vector.scalar_tensor_tensor(
                     out=junkv[:], in0=xs, scalar=1.0, in1=xs,
                     op0=ALU.mult, op1=ALU.mult, accum_out=ss[:, m : m + 1],
                 )
 
-        def log_map(h):
-            lo, hi = GT * h, GT * (h + 1)
-            a, r = 2 * GT * h, 2 * GT * h + GT
-            nc.gpsimd.tensor_scalar(
-                out=v[:, lo:hi], in0=xr3[:, lo:hi, PAD - 1], scalar1=1.0 + 1e-7,
-                scalar2=None, op0=ALU.max,
+        def radicands():
+            nc.vector.tensor_scalar_max(out=v[:], in0=xr3[:, :, PAD - 1], scalar1=1.0 + 1e-7)
+            nc.vector.tensor_scalar_add(out=vp1[:], in0=v[:], scalar1=1.0)
+            nc.vector.scalar_tensor_tensor(
+                out=radicand[:, NT : 2 * NT], in0=v[:], scalar=-1.0, in1=vp1[:],
+                op0=ALU.add, op1=ALU.mult,
             )
-            nc.gpsimd.tensor_scalar(
-                out=vm1[:, lo:hi], in0=v[:, lo:hi], scalar1=-1.0, scalar2=None, op0=ALU.add
-            )
-            nc.gpsimd.tensor_scalar(
-                out=vp1[:, lo:hi], in0=v[:, lo:hi], scalar1=1.0, scalar2=None, op0=ALU.add
-            )
-            nc.gpsimd.tensor_tensor(
-                out=radicand[:, r : r + GT], in0=vm1[:, lo:hi], in1=vp1[:, lo:hi], op=ALU.mult
-            )
-            nc.gpsimd.tensor_scalar(
-                out=radicand[:, a : a + GT], in0=ss[:, lo:hi], scalar1=1e-14,
-                scalar2=None, op0=ALU.max,
-            )
-            nc.gpsimd.tensor_tensor(
-                out=root[:, a : a + 2 * GT], in0=radicand[:, a : a + 2 * GT],
-                in1=half[:], op=ALU.pow,
-            )
-            nc.gpsimd.tensor_tensor(
-                out=warg[:, lo:hi], in0=v[:, lo:hi], in1=root[:, r : r + GT], op=ALU.add
-            )
-            nc.scalar.activation(out=dist[:, lo:hi], in_=warg[:, lo:hi], func=ACT.Ln)
-            nc.gpsimd.tensor_tensor(
-                out=sx[:, lo:hi], in0=root[:, a : a + GT], in1=dist[:, lo:hi], op=ALU.mult
-            )
+
+        def roots():
+            nc.vector.tensor_scalar_max(out=radicand[:, 0:NT], in0=ss[:], scalar1=1e-14)
+            nc.scalar.activation(out=root[:], in_=radicand[:], func=ACT.Sqrt)
+            nc.vector.tensor_tensor(out=warg[:], in0=v[:], in1=root[:, NT : 2 * NT], op=ALU.add)
+            nc.vector.reciprocal(out=rns[:], in_=root[:, 0:NT])
+
+        def factors():
+            nc.scalar.activation(out=dist[:], in_=warg[:], func=ACT.Ln)
+            nc.vector.tensor_tensor(out=sx[:], in0=rns[:], in1=dist[:], op=ALU.mult)
 
         def scale_x(m):
             ts = tpool.tile([P, 1024], BF16, align_bytes=64, name="ts")
@@ -207,7 +201,6 @@ def tile_lorentzmlp_pa_kernel(tc, x_hyp, W, b, out):
             )
 
         ot_t = {}
-        acc_t = {}
         ps_t = {}
 
         def multiply(m, c):
@@ -236,17 +229,14 @@ def tile_lorentzmlp_pa_kernel(tc, x_hyp, W, b, out):
             )
 
         def square(m, lo, hi, j):
-            if m not in acc_t:
-                acc = small.tile([P, 8], F32, name="acc")
-                acc_t[m] = acc
             junk = spool.tile([P, 1024], BF16, name="junk")
             nc.scalar.activation(
                 out=junk[:, 0 : hi - lo], in_=columns(m, lo, hi),
-                func=ACT.Square, accum_out=acc_t[m][:, j : j + 1],
+                func=ACT.Square, accum_out=acc[:, 6 * m + j : 6 * m + j + 1],
             )
 
         n2_t = {}
-        nr_t = {}
+        rn_t = {}
         ncl_t = {}
         ep_t = {}
         em_t = {}
@@ -278,132 +268,129 @@ def tile_lorentzmlp_pa_kernel(tc, x_hyp, W, b, out):
                 in_=ot_t[m][:, OPAD - 1 + lo : OPAD - 1 + hi],
             )
 
-        def norm_sum(m, parts):
+        def norm_sum(m):
             n2 = small.tile([P, 1], F32, name="n2")
-            junk8 = small.tile([P, 8], F32, name="junk8")
+            junk8 = small.tile([P, 6], F32, name="junk8")
             nc.scalar.activation(
-                out=junk8[:, 0:parts], in_=acc_t[m][:, 0:parts], func=ACT.Copy,
+                out=junk8[:], in_=acc[:, 6 * m : 6 * m + 6], func=ACT.Copy, scale=4.0,
                 accum_out=n2[:],
             )
             n2_t[m] = n2
 
         def norm_root(m):
-            pr = small.tile([P, 2], F32, name="pr")
-            nc.gpsimd.tensor_scalar(
-                out=pr[:], in0=n2_t[m][:].to_broadcast([P, 2]), scalar1=1e-14,
-                scalar2=None, op0=ALU.max,
-            )
-            nr = small.tile([P, 2], F32, name="nr")
-            nc.gpsimd.tensor_tensor(
-                out=nr[:], in0=pr[:], in1=half[:, GT - 1 : GT + 1], op=ALU.pow
-            )
+            rn = small.tile([P, 1], F32, name="rn")
+            nc.gpsimd.tensor_tensor(out=rn[:], in0=n2_t[m][:], in1=mhalf[:], op=ALU.pow)
+            rn_t[m] = rn
+
+        def norm_clamp(m):
             ncl = small.tile([P, 1], F32, name="ncl")
-            nc.gpsimd.tensor_scalar(
-                out=ncl[:], in0=nr[:, 1:2], scalar1=10.0, scalar2=None, op0=ALU.min
+            nc.vector.tensor_scalar(
+                out=ncl[:], in0=n2_t[m][:], scalar1=rn_t[m][:, 0:1], scalar2=20.0,
+                op0=ALU.mult, op1=ALU.min,
             )
-            nr_t[m] = nr
             ncl_t[m] = ncl
 
         def norm_exp(m):
             ep = small.tile([P, 1], F32, name="ep")
-            nc.scalar.activation(out=ep[:], in_=ncl_t[m][:], func=ACT.Exp)
+            nc.scalar.activation(out=ep[:], in_=ncl_t[m][:], func=ACT.Exp, scale=0.5)
             em = small.tile([P, 1], F32, name="em")
-            nc.scalar.activation(out=em[:], in_=ncl_t[m][:], func=ACT.Exp, scale=-1.0)
+            nc.scalar.activation(out=em[:], in_=ncl_t[m][:], func=ACT.Exp, scale=-0.5)
             ep_t[m] = ep
             em_t[m] = em
 
         def norm_end(m):
-            sh = small.tile([P, 1], F32, name="sh")
-            nc.vector.tensor_scalar(
-                out=sh[:], in0=ep_t[m][:], scalar1=em_t[m][:, 0:1], scalar2=0.5,
+            sc = small.tile([P, 1], F32, name="sc")
+            nc.vector.scalar_tensor_tensor(
+                out=sc[:], in0=ep_t[m][:], scalar=em_t[m][:, 0:1], in1=rn_t[m][:],
                 op0=ALU.subtract, op1=ALU.mult,
             )
             nc.vector.tensor_scalar(
                 out=ot_t[m][:, OPAD - 1 : OPAD], in0=ep_t[m][:],
                 scalar1=em_t[m][:, 0:1], scalar2=0.5, op0=ALU.add, op1=ALU.mult,
             )
-            sc = small.tile([P, 1], F32, name="sc")
-            nc.vector.tensor_scalar(
-                out=sc[:], in0=sh[:], scalar1=nr_t[m][:, 0:1], scalar2=None, op0=ALU.mult
-            )
             sc_t[m] = sc
 
         load_w(0)
         load_x(0)
         load_w(1)
-        load_x(1)
-        load_bias(0)
         load_w(2)
         load_w(3)
         make_identity(nc, ident_f[:])
         nc.vector.memset(one[:], 1.0)
-        nc.vector.memset(half[:, 0:GT], -0.5)
-        nc.vector.memset(half[:, GT : 2 * GT], 0.5)
-        nc.scalar.activation(out=warm[:, 0:1], in_=one[:], func=ACT.Ln)
+        nc.vector.memset(mhalf[:], -0.5)
+        nc.vector.memset(acc[:], 2e-15)
+        nc.scalar.activation(out=warm[:, 0:1], in_=one[:], func=ACT.Sqrt)
 
-        for s in range(NCH):
-            transpose_w(s)
-            if 1 <= s <= 4:
-                transpose_x(2 * s - 2)
-                transpose_x(2 * s - 1)
-            if s + WBUFS < NCH:
-                load_w(s + WBUFS)
-            if s == 1:
-                load_bias(1)
-            copy_w(s)
-            for c in range(NCH):
-                if c == s - 2 and c >= 1 or c == 0 and s == 3:
-                    evict(0, c)
-                    if c % 2 == 1:
-                        square(0, 512 * (c - 1), 512 * (c + 1), c // 2)
-            if s <= 1:
-                for m in range(GT * s, GT * (s + 1)):
-                    row_norm(m)
-                log_map(s)
-            quantise_w(s)
-            if 1 <= s <= 4:
-                regroup_x(2 * s - 2)
-                regroup_x(2 * s - 1)
-                quantise_x(2 * s - 2)
-                quantise_x(2 * s - 1)
-            if s <= 1:
-                for m in range(GT * s, GT * (s + 1)):
-                    scale_x(m)
-            if s == 2:
-                nc.scalar.activation(out=warm[:, 1:2], in_=one[:], func=ACT.Exp)
-                multiply(0, 0)
-            if s >= 2:
-                multiply(0, s - 1)
-
-        order = [(1, 0), (1, 1), (0, 7)]
-        order += [(1, c) for c in range(2, NCH)]
-        order += [(m, c) for m in range(2, NT) for c in range(NCH)]
-        evict(0, 6)
-        last = NT - 1
-        for m, c in order:
-            multiply(m, c)
+        def bank(m, c):
             evict(m, c)
-            if m == last and c >= NCH - 2:
+            if m == NT - 1 and c >= NCH - 2:
                 square(m, 512 * c, 512 * (c + 1), c - NCH + 5)
             elif c % 2 == 1:
                 square(m, 512 * (c - 1), 512 * (c + 1), c // 2)
-            if c == NCH - 1:
-                norm_sum(m, 5 if m == last else 4)
-                norm_root(m)
-                norm_exp(m)
-                if 1 <= m < last:
-                    scale_on_gpsimd(m - 1, 3072, 4096)
-                    store(m - 1, 2049, 4097)
-            if m >= 1 and c == (4 if m == 1 else 3):
+
+        for s in range(NCH):
+            transpose_w(s)
+            if XS <= s < XS + len(XSCHED):
+                for m in XSCHED[s - XS]:
+                    transpose_x(m)
+            if s + WBUFS < NCH:
+                load_w(s + WBUFS)
+            if s in (2, 3):
+                load_bias(s - 2)
+            copy_w(s)
+            if s == 0:
+                for m in range(NT):
+                    row_norm(m)
+                    if m == NT - 1:
+                        radicands()
+                roots()
+            if s == 0:
+                factors()
+                quantise_w(0)
+                for m in range(4):
+                    scale_x(m)
+            else:
+                quantise_w(s)
+            if XS <= s < XS + len(XSCHED):
+                for m in XSCHED[s - XS]:
+                    regroup_x(m)
+                for m in XSCHED[s - XS]:
+                    quantise_x(m)
+            if XS <= s < XS + 2:
+                for m in (0, 1):
+                    scale_x(4 + 2 * (s - XS) + m)
+            if s == 3:
+                nc.scalar.activation(out=warm[:, 1:2], in_=one[:], func=ACT.Exp)
+
+        order = [(m, c) for m in range(NT) for c in range(NCH)]
+        last = NT - 1
+        for m, c in order:
+            multiply(m, c)
+            if m >= 1 and c == CLAMP:
+                norm_clamp(m - 1)
+                norm_exp(m - 1)
+            if m >= 1 and c == ROOT:
+                norm_root(m - 1)
+            if m >= 2 and c == Q3:
+                scale_on_gpsimd(m - 2, 2048, GE)
+                if GE < 4096:
+                    scale_on_scalar(m - 2, GE, 4096)
+                store(m - 2, 2049, 4097)
+            if m >= 1 and c == (LEND if m == last else END):
                 norm_end(m - 1)
-                scale_on_gpsimd(m - 1, 0, 1024)
-                scale_on_gpsimd(m - 1, 1024, 2048)
+                scale_on_gpsimd(m - 1, 0, 2048)
                 store(m - 1, 0, 2049)
-                scale_on_gpsimd(m - 1, 2048, 3072)
+            bank(m, c)
+            if c == NCH - 1:
+                norm_sum(m)
 
         m = last
-        scale_on_vector(m - 1, 3072, 4096)
+        norm_root(m)
+        scale_on_scalar(m - 1, 3072, 4096)
+        scale_on_vector(m - 1, 2048, 3072)
         store(m - 1, 2049, 4097)
+        norm_clamp(m)
+        norm_exp(m)
         norm_end(m)
         scale_on_vector(m, 0, 1024)
         store(m, 0, 1025)

@@ -21,7 +21,7 @@ XP = PAD + 1024
 WP = XP // 2
 OPAD = 8
 WBUFS = 4
-NORM_S = (0, 2, 4)
+NORM_S = (0, 2, 4, 6)
 OB = 5
 XS = 2
 XSCHED = ((0, 1), (2, 3), (4, 5), (6, 7))
@@ -80,8 +80,8 @@ def tile_lorentzmlp_pa_kernel(tc, x_hyp, W, b, out):
             dst = wraw[:].rearrange("p (t k) -> p t k", k=XP)
             for tp in range(2):
                 nc.sync.dma_start(
-                    out=dst[:, 2 * tp : 2 * tp + 2, PAD - 1 : XP],
-                    in_=wsrc[c][:, 2 * tp : 2 * tp + 2, :],
+                    out=dst[:, 2 * tp : 2 * tp + 2, PAD:XP],
+                    in_=wsrc[c][:, 2 * tp : 2 * tp + 2, 1:1025],
                 )
             wraw_t[c] = wraw
 
@@ -335,8 +335,9 @@ def tile_lorentzmlp_pa_kernel(tc, x_hyp, W, b, out):
                     transpose_x(m)
             if s + WBUFS < NCH:
                 load_w(s + WBUFS)
-            if s in (2, 3):
-                load_bias(s - 2)
+            if s + WBUFS == NCH - 1:
+                load_bias(0)
+                load_bias(1)
             copy_w(s)
             if s == 0:
                 for m in range(NT):

@@ -20,6 +20,7 @@ PAD = 32
 XP = PAD + 1024
 WP = XP // 2
 OPAD = 8
+X2 = 2080
 WBUFS = 4
 NORM_S = (0, 2, 4, 6)
 OB = 5
@@ -44,9 +45,11 @@ def tile_lorentzmlp_pa_kernel(tc, x_hyp, W, b, out):
         small = ctx.enter_context(tc.tile_pool(name="small", bufs=3))
         psum = ctx.enter_context(tc.psum_pool(name="psum", bufs=8))
 
-        xraw = const.tile([P, NT * XP], BF16, align_bytes=64)
-        xr3 = xraw[:].rearrange("p (m c) -> p m c", c=XP)
-        xsrc = x_hyp.rearrange("(m p) c -> p m c", p=P)
+        xraw = const.tile([P, NT // 2 * X2], BF16, align_bytes=64)
+        xpair = xraw[:].rearrange("p (h r) -> p h r", r=X2)[:, :, 0 : 2 * 1025]
+        xr4 = xpair.rearrange("p h (j c) -> p h j c", c=1025)
+        xsrc = x_hyp.rearrange("(p m) c -> p (m c)", m=NT)
+        osrc = out.rearrange("(p m) c -> m p c", m=NT)
         wsrc = W[1:4097, :].rearrange("(c t p) k -> c p t k", t=4, p=P)
         xq = const.tile([P, NT * 256], U32, align_bytes=64)
         xsc = const.tile([P, NT * 256], U8, align_bytes=64)
@@ -88,17 +91,18 @@ def tile_lorentzmlp_pa_kernel(tc, x_hyp, W, b, out):
         def load_x(h):
             for m in range(0, NT, 2):
                 nc.sync.dma_start(
-                    out=xr3[:, m : m + 2, PAD - 1 : XP], in_=xsrc[:, m : m + 2, :]
+                    out=xpair[:, m // 2, :],
+                    in_=xsrc[:, 1025 * m : 1025 * (m + 2)],
                 )
 
         def load_bias(h):
             nc.sync.dma_start(
-                out=bias[:, 2048 * h : 2048 * (h + 1)],
-                in_=b[1 + 2048 * h : 1 + 2048 * (h + 1)].partition_broadcast(P),
+                out=bias[:, 1024 * h : 1024 * (h + 1)],
+                in_=b[1 + 1024 * h : 1 + 1024 * (h + 1)].partition_broadcast(P),
             )
 
         def row_norm(m):
-            xs = xr3[:, m, PAD:XP]
+            xs = xr4[:, m // 2, m % 2, 1:1025]
             if m in NORM_S:
                 junk = spool.tile([P, 1024], BF16, name="junk")
                 nc.scalar.activation(
@@ -112,7 +116,10 @@ def tile_lorentzmlp_pa_kernel(tc, x_hyp, W, b, out):
                 )
 
         def radicands():
-            nc.vector.tensor_scalar_max(out=v[:], in0=xr3[:, :, PAD - 1], scalar1=1.0 + 1e-7)
+            nc.vector.tensor_scalar_max(
+                out=v[:].rearrange("p (h j) -> p h j", j=2), in0=xr4[:, :, :, 0],
+                scalar1=1.0 + 1e-7,
+            )
             nc.vector.tensor_scalar_add(out=vp1[:], in0=v[:], scalar1=1.0)
             nc.vector.scalar_tensor_tensor(
                 out=radicand[:, NT : 2 * NT], in0=v[:], scalar=-1.0, in1=vp1[:],
@@ -132,7 +139,7 @@ def tile_lorentzmlp_pa_kernel(tc, x_hyp, W, b, out):
         def scale_x(m):
             ts = tpool.tile([P, 1024], BF16, align_bytes=64, name="ts")
             nc.vector.tensor_scalar(
-                out=ts[:], in0=xr3[:, m, PAD:XP], scalar1=sx[:, m : m + 1],
+                out=ts[:], in0=xr4[:, m // 2, m % 2, 1:1025], scalar1=sx[:, m : m + 1],
                 scalar2=None, op0=ALU.mult,
             )
             ts_t[m] = ts
@@ -264,7 +271,7 @@ def tile_lorentzmlp_pa_kernel(tc, x_hyp, W, b, out):
 
         def store(m, lo, hi):
             nc.sync.dma_start(
-                out=out[m * P : (m + 1) * P, lo:hi],
+                out=osrc[m][:, lo:hi],
                 in_=ot_t[m][:, OPAD - 1 + lo : OPAD - 1 + hi],
             )
 
@@ -336,8 +343,8 @@ def tile_lorentzmlp_pa_kernel(tc, x_hyp, W, b, out):
             if s + WBUFS < NCH:
                 load_w(s + WBUFS)
             if s + WBUFS == NCH - 1:
-                load_bias(0)
-                load_bias(1)
+                for h in range(4):
+                    load_bias(h)
             copy_w(s)
             if s == 0:
                 for m in range(NT):
@@ -376,11 +383,11 @@ def tile_lorentzmlp_pa_kernel(tc, x_hyp, W, b, out):
                 scale_on_gpsimd(m - 2, 2048, GE)
                 if GE < 4096:
                     scale_on_scalar(m - 2, GE, 4096)
-                store(m - 2, 2049, 4097)
+                store(m - 2, 2048 - (m - 2), 4097)
             if m >= 1 and c == (LEND if m == last else END):
                 norm_end(m - 1)
                 scale_on_gpsimd(m - 1, 0, 2048)
-                store(m - 1, 0, 2049)
+                store(m - 1, 0, 2048 - (m - 1))
             bank(m, c)
             if c == NCH - 1:
                 norm_sum(m)
@@ -389,15 +396,15 @@ def tile_lorentzmlp_pa_kernel(tc, x_hyp, W, b, out):
         norm_root(m)
         scale_on_scalar(m - 1, 3072, 4096)
         scale_on_vector(m - 1, 2048, 3072)
-        store(m - 1, 2049, 4097)
+        store(m - 1, 2048 - (m - 1), 4097)
         norm_clamp(m)
         norm_exp(m)
         norm_end(m)
         scale_on_vector(m, 0, 1024)
-        store(m, 0, 1025)
+        store(m, 0, 1024 - m)
         scale_on_vector(m, 1024, 2048)
-        store(m, 1025, 2049)
+        store(m, 1024 - m, 2048 - m)
         scale_on_scalar(m, 2048, 3072)
-        store(m, 2049, 3073)
+        store(m, 2048 - m, 3072 - m)
         scale_on_vector(m, 3072, 4096)
-        store(m, 3073, 4097)
+        store(m, 3072 - m, 4097)

@@ -27,7 +27,7 @@ OB = 5
 XS = 2
 XSCHED = ((0, 1), (2, 3), (4, 5), (6, 7))
 ROOT, Q3, CLAMP, END = 1, 1, 3, 6
-GE = 3968
+GE, VE = 3328, 3840
 LEND = 5
 GT = 4
 
@@ -381,8 +381,8 @@ def tile_lorentzmlp_pa_kernel(tc, x_hyp, W, b, out):
                 norm_root(m - 1)
             if m >= 2 and c == Q3:
                 scale_on_gpsimd(m - 2, 2048, GE)
-                if GE < 4096:
-                    scale_on_scalar(m - 2, GE, 4096)
+                scale_on_vector(m - 2, GE, VE)
+                scale_on_scalar(m - 2, VE, 4096)
                 store(m - 2, 2048 - (m - 2), 4097)
             if m >= 1 and c == (LEND if m == last else END):
                 norm_end(m - 1)

@@ -19,17 +19,11 @@ NCH = 8
 PAD = 32
 XP = PAD + 1024
 WP = XP // 2
-OPAD = 8
 X2 = 2080
-WBUFS = 4
-NORM_S = (0, 2, 4, 6)
-OB = 5
-XS = 2
-XSCHED = ((0, 1), (2, 3), (4, 5), (6, 7))
-ROOT, Q3, CLAMP, END = 1, 1, 3, 6
+OPAD = 8
+WBUFS = 6
+NSUM = 5
 GE, VE = 3328, 3840
-LEND = 5
-GT = 4
 
 
 def tile_lorentzmlp_pa_kernel(tc, x_hyp, W, b, out):
@@ -39,9 +33,9 @@ def tile_lorentzmlp_pa_kernel(tc, x_hyp, W, b, out):
         const = ctx.enter_context(tc.tile_pool(name="const", bufs=1))
         wpool = ctx.enter_context(tc.tile_pool(name="wraw", bufs=WBUFS))
         gpool = ctx.enter_context(tc.tile_pool(name="grouped", bufs=2))
-        tpool = ctx.enter_context(tc.tile_pool(name="ts", bufs=4))
+        tpool = ctx.enter_context(tc.tile_pool(name="ts", bufs=NT))
         spool = ctx.enter_context(tc.tile_pool(name="scratch", bufs=2))
-        opool = ctx.enter_context(tc.tile_pool(name="outs", bufs=OB))
+        opool = ctx.enter_context(tc.tile_pool(name="outs", bufs=4))
         small = ctx.enter_context(tc.tile_pool(name="small", bufs=3))
         psum = ctx.enter_context(tc.psum_pool(name="psum", bufs=8))
 
@@ -49,25 +43,25 @@ def tile_lorentzmlp_pa_kernel(tc, x_hyp, W, b, out):
         xpair = xraw[:].rearrange("p (h r) -> p h r", r=X2)[:, :, 0 : 2 * 1025]
         xr4 = xpair.rearrange("p h (j c) -> p h j c", c=1025)
         xsrc = x_hyp.rearrange("(p m) c -> p (m c)", m=NT)
-        osrc = out.rearrange("(p m) c -> m p c", m=NT)
         wsrc = W[1:4097, :].rearrange("(c t p) k -> c p t k", t=4, p=P)
+        odst = out.rearrange("(p m) c -> m p c", m=NT)
         xq = const.tile([P, NT * 256], U32, align_bytes=64)
         xsc = const.tile([P, NT * 256], U8, align_bytes=64)
         wq = const.tile([P, NCH * 1024], U32, align_bytes=64)
         wsc = const.tile([P, NCH * 1024], U8, align_bytes=64)
         bias = const.tile([P, 4096], BF16)
-        ident_f = const.tile([P, P], F32)
+        ident = const.tile([P, P], F32)
         one = const.tile([P, 1], F32)
         mhalf = const.tile([P, 1], F32)
-        acc = const.tile([P, 6 * NT], F32)
         warm = const.tile([P, 2], F32)
+        acc = const.tile([P, NT * NSUM], F32)
         ss = const.tile([P, NT], F32)
         v = const.tile([P, NT], F32)
         vp1 = const.tile([P, NT], F32)
         radicand = const.tile([P, 2 * NT], F32)
         root = const.tile([P, 2 * NT], F32)
-        rns = const.tile([P, NT], F32)
         warg = const.tile([P, NT], F32)
+        rns = const.tile([P, NT], F32)
         dist = const.tile([P, NT], F32)
         sx = const.tile([P, NT], F32)
 
@@ -77,6 +71,12 @@ def tile_lorentzmlp_pa_kernel(tc, x_hyp, W, b, out):
         ts_t = {}
         xbank = {}
         xg_t = {}
+
+        def load_x():
+            for h in range(NT // 2):
+                nc.sync.dma_start(
+                    out=xpair[:, h, :], in_=xsrc[:, 2050 * h : 2050 * (h + 1)]
+                )
 
         def load_w(c):
             wraw = wpool.tile([P, 4 * XP], BF16, align_bytes=64, name="wraw")
@@ -88,34 +88,27 @@ def tile_lorentzmlp_pa_kernel(tc, x_hyp, W, b, out):
                 )
             wraw_t[c] = wraw
 
-        def load_x(h):
-            for m in range(0, NT, 2):
+        def load_bias():
+            for h in range(4):
                 nc.sync.dma_start(
-                    out=xpair[:, m // 2, :],
-                    in_=xsrc[:, 1025 * m : 1025 * (m + 2)],
+                    out=bias[:, 1024 * h : 1024 * (h + 1)],
+                    in_=b[1 + 1024 * h : 1 + 1024 * (h + 1)].partition_broadcast(P),
                 )
-
-        def load_bias(h):
-            nc.sync.dma_start(
-                out=bias[:, 1024 * h : 1024 * (h + 1)],
-                in_=b[1 + 1024 * h : 1 + 1024 * (h + 1)].partition_broadcast(P),
-            )
 
         def row_norm(m):
             xs = xr4[:, m // 2, m % 2, 1:1025]
-            if m in NORM_S:
-                junk = spool.tile([P, 1024], BF16, name="junk")
+            junk = spool.tile([P, 1024], BF16, name="junk" if m % 2 == 0 else "junkv")
+            if m % 2 == 0:
                 nc.scalar.activation(
                     out=junk[:], in_=xs, func=ACT.Square, accum_out=ss[:, m : m + 1]
                 )
             else:
-                junkv = spool.tile([P, 1024], BF16, name="junkv")
                 nc.vector.scalar_tensor_tensor(
-                    out=junkv[:], in0=xs, scalar=1.0, in1=xs,
+                    out=junk[:], in0=xs, scalar=1.0, in1=xs,
                     op0=ALU.mult, op1=ALU.mult, accum_out=ss[:, m : m + 1],
                 )
 
-        def radicands():
+        def log_map():
             nc.vector.tensor_scalar_max(
                 out=v[:].rearrange("p (h j) -> p h j", j=2), in0=xr4[:, :, :, 0],
                 scalar1=1.0 + 1e-7,
@@ -125,14 +118,12 @@ def tile_lorentzmlp_pa_kernel(tc, x_hyp, W, b, out):
                 out=radicand[:, NT : 2 * NT], in0=v[:], scalar=-1.0, in1=vp1[:],
                 op0=ALU.add, op1=ALU.mult,
             )
-
-        def roots():
             nc.vector.tensor_scalar_max(out=radicand[:, 0:NT], in0=ss[:], scalar1=1e-14)
             nc.scalar.activation(out=root[:], in_=radicand[:], func=ACT.Sqrt)
-            nc.vector.tensor_tensor(out=warg[:], in0=v[:], in1=root[:, NT : 2 * NT], op=ALU.add)
+            nc.vector.tensor_tensor(
+                out=warg[:], in0=v[:], in1=root[:, NT : 2 * NT], op=ALU.add
+            )
             nc.vector.reciprocal(out=rns[:], in_=root[:, 0:NT])
-
-        def factors():
             nc.scalar.activation(out=dist[:], in_=warg[:], func=ACT.Ln)
             nc.vector.tensor_tensor(out=sx[:], in0=rns[:], in1=dist[:], op=ALU.mult)
 
@@ -151,18 +142,18 @@ def tile_lorentzmlp_pa_kernel(tc, x_hyp, W, b, out):
                 for u in range(2):
                     col = (g * 2 + u) * P
                     nc.tensor.transpose(
-                        xt[:, col : col + P],
-                        words[:, 256 * g + u : 256 * (g + 1) : 2],
-                        ident_f[:],
+                        xt[:, col : col + P], words[:, 256 * g + u : 256 * (g + 1) : 2], ident[:]
                     )
             xbank[m] = xt
 
         def regroup_x(m):
             xg = gpool.tile([P, 1024], BF16, align_bytes=64, name="xg")
-            nc.vector.tensor_copy(
-                out=xg[:].bitcast(F32).rearrange("p (g r u) -> p g r u", g=2, u=2),
-                in_=xbank[m][:].rearrange("p (g u r) -> p g r u", g=2, u=2),
-            )
+            dst = xg[:].bitcast(F32).rearrange("p (g r u) -> p g r u", g=2, u=2)
+            src = xbank[m][:].rearrange("p (g u r) -> p g r u", g=2, u=2)
+            if m % 2 == 0:
+                nc.vector.tensor_copy(out=dst, in_=src)
+            else:
+                nc.scalar.copy(out=dst, in_=src)
             xg_t[m] = xg
 
         def quantise_x(m):
@@ -172,27 +163,25 @@ def tile_lorentzmlp_pa_kernel(tc, x_hyp, W, b, out):
                 in_=xg_t[m][:],
             )
 
-        def transpose_w(c):
+        def transpose_w(c, tp):
             wf = wraw_t[c][:].bitcast(F32)
-            for tp in range(2):
-                for g in range(2):
-                    wt = psum.tile([P, 512], F32, tag="bank", name="wt")
-                    for tl in range(2):
-                        for u in range(2):
-                            col = (tl * 2 + u) * P
-                            src = (2 * tp + tl) * WP + PAD // 2 + 256 * g
-                            nc.tensor.transpose(
-                                wt[:, col : col + P],
-                                wf[:, src + u : src + 256 : 2],
-                                ident_f[:],
-                            )
-                    wbank[(c, 2 * g + tp)] = wt
+            for g in range(2):
+                wt = psum.tile([P, 512], F32, tag="bank", name="wt")
+                for tl in range(2):
+                    for u in range(2):
+                        col = (tl * 2 + u) * P
+                        src = (2 * tp + tl) * WP + PAD // 2 + 256 * g
+                        nc.tensor.transpose(
+                            wt[:, col : col + P], wf[:, src + u : src + 256 : 2], ident[:]
+                        )
+                wbank[(c, 2 * g + tp)] = wt
 
-        def copy_w(c):
-            wg = gpool.tile([P, 4096], BF16, align_bytes=64, name="wg")
-            wg_t[c] = wg
-            wgf = wg[:].bitcast(F32)
-            for k in (0, 2, 1, 3):
+        def copy_w(c, tp):
+            if tp == 0:
+                wg = gpool.tile([P, 4096], BF16, align_bytes=64, name="wg")
+                wg_t[c] = wg
+            wgf = wg_t[c][:].bitcast(F32)
+            for k in (tp, 2 + tp):
                 nc.scalar.copy(
                     out=wgf[:, k * 512 : (k + 1) * 512].rearrange(
                         "p (tl n u) -> p tl n u", tl=2, u=2
@@ -207,8 +196,48 @@ def tile_lorentzmlp_pa_kernel(tc, x_hyp, W, b, out):
                 in_=wg_t[c][:],
             )
 
+        load_x()
+        for c in range(WBUFS):
+            load_w(c)
+        make_identity(nc, ident[:])
+        nc.vector.memset(one[:], 1.0)
+        nc.vector.memset(mhalf[:], -0.5)
+        nc.vector.memset(acc[:], 2e-15)
+        nc.scalar.activation(out=warm[:, 0:1], in_=one[:], func=ACT.Sqrt)
+        for m in range(NT):
+            row_norm(m)
+        log_map()
+        for m in range(NT):
+            scale_x(m)
+        for c in range(NCH):
+            riders = range(max(0, 2 * c - 5), max(0, min(NT, 2 * c - 3)))
+            for tp in range(2):
+                transpose_w(c, tp)
+                copy_w(c, tp)
+            for m in riders:
+                transpose_x(m)
+            if c + WBUFS < NCH:
+                load_w(c + WBUFS)
+            if c + WBUFS == NCH - 1:
+                load_bias()
+            quantise_w(c)
+            for m in riders:
+                regroup_x(m)
+            for m in riders:
+                quantise_x(m)
+        nc.scalar.activation(out=warm[:, 1:2], in_=one[:], func=ACT.Exp)
+
+        last = NT - 1
         ot_t = {}
-        ps_t = {}
+        n2_t = {}
+        rn_t = {}
+        ncl_t = {}
+        ep_t = {}
+        em_t = {}
+        sc_t = {}
+
+        def columns(m, lo, hi):
+            return ot_t[m][:, OPAD + lo : OPAD + hi]
 
         def multiply(m, c):
             ps = psum.tile([P, 512], F32, tag="bank", name="ps")
@@ -224,33 +253,62 @@ def tile_lorentzmlp_pa_kernel(tc, x_hyp, W, b, out):
                     start=(g == 0),
                     stop=(g == 1),
                 )
-            ps_t[(m, c)] = ps
+            return ps
 
-        def evict(m, c):
-            if m not in ot_t:
+        def add_bias(m, c, ps):
+            if c == 0:
                 ot = opool.tile([P, OPAD + 4096], F32, name="ot")
                 ot_t[m] = ot
             nc.vector.tensor_tensor(
-                out=columns(m, 512 * c, 512 * (c + 1)), in0=ps_t[(m, c)][:],
+                out=columns(m, 512 * c, 512 * (c + 1)), in0=ps[:],
                 in1=bias[:, 512 * c : 512 * (c + 1)], op=ALU.add,
             )
 
         def square(m, lo, hi, j):
             junk = spool.tile([P, 1024], BF16, name="junk")
             nc.scalar.activation(
-                out=junk[:, 0 : hi - lo], in_=columns(m, lo, hi),
-                func=ACT.Square, accum_out=acc[:, 6 * m + j : 6 * m + j + 1],
+                out=junk[:, 0 : hi - lo], in_=columns(m, lo, hi), func=ACT.Square,
+                accum_out=acc[:, NSUM * m + j : NSUM * m + j + 1],
             )
 
-        n2_t = {}
-        rn_t = {}
-        ncl_t = {}
-        ep_t = {}
-        em_t = {}
-        sc_t = {}
+        def norm_sum(m):
+            n2 = small.tile([P, 1], F32, name="n2")
+            junk5 = small.tile([P, NSUM], F32, name="junk5")
+            nc.scalar.activation(
+                out=junk5[:], in_=acc[:, NSUM * m : NSUM * (m + 1)], func=ACT.Copy,
+                scale=4.0, accum_out=n2[:],
+            )
+            n2_t[m] = n2
 
-        def columns(m, lo, hi):
-            return ot_t[m][:, OPAD + lo : OPAD + hi]
+        def norm_root(m):
+            rn = small.tile([P, 1], F32, name="rn")
+            nc.gpsimd.tensor_tensor(out=rn[:], in0=n2_t[m][:], in1=mhalf[:], op=ALU.pow)
+            rn_t[m] = rn
+
+        def norm_exp(m):
+            ncl = small.tile([P, 1], F32, name="ncl")
+            nc.vector.tensor_scalar(
+                out=ncl[:], in0=n2_t[m][:], scalar1=rn_t[m][:, 0:1], scalar2=20.0,
+                op0=ALU.mult, op1=ALU.min,
+            )
+            ep = small.tile([P, 1], F32, name="ep")
+            nc.scalar.activation(out=ep[:], in_=ncl[:], func=ACT.Exp, scale=0.5)
+            em = small.tile([P, 1], F32, name="em")
+            nc.scalar.activation(out=em[:], in_=ncl[:], func=ACT.Exp, scale=-0.5)
+            ep_t[m] = ep
+            em_t[m] = em
+
+        def factors(m):
+            sc = small.tile([P, 1], F32, name="sc")
+            nc.vector.scalar_tensor_tensor(
+                out=sc[:], in0=ep_t[m][:], scalar=em_t[m][:, 0:1], in1=rn_t[m][:],
+                op0=ALU.subtract, op1=ALU.mult,
+            )
+            nc.gpsimd.tensor_scalar(
+                out=ot_t[m][:, OPAD - 1 : OPAD], in0=ep_t[m][:],
+                scalar1=em_t[m][:, 0:1], scalar2=0.5, op0=ALU.add, op1=ALU.mult,
+            )
+            sc_t[m] = sc
 
         def scale_on_gpsimd(m, lo, hi):
             seg = columns(m, lo, hi)
@@ -271,135 +329,45 @@ def tile_lorentzmlp_pa_kernel(tc, x_hyp, W, b, out):
 
         def store(m, lo, hi):
             nc.sync.dma_start(
-                out=osrc[m][:, lo:hi],
-                in_=ot_t[m][:, OPAD - 1 + lo : OPAD - 1 + hi],
+                out=odst[m][:, lo:hi], in_=ot_t[m][:, OPAD - 1 + lo : OPAD - 1 + hi]
             )
 
-        def norm_sum(m):
-            n2 = small.tile([P, 1], F32, name="n2")
-            junk8 = small.tile([P, 6], F32, name="junk8")
-            nc.scalar.activation(
-                out=junk8[:], in_=acc[:, 6 * m : 6 * m + 6], func=ACT.Copy, scale=4.0,
-                accum_out=n2[:],
-            )
-            n2_t[m] = n2
+        def first_half(m):
+            factors(m)
+            scale_on_gpsimd(m, 0, 2048)
+            store(m, 0, 2048 - m)
 
-        def norm_root(m):
-            rn = small.tile([P, 1], F32, name="rn")
-            nc.gpsimd.tensor_tensor(out=rn[:], in0=n2_t[m][:], in1=mhalf[:], op=ALU.pow)
-            rn_t[m] = rn
+        def second_half(m):
+            scale_on_gpsimd(m, 2048, GE)
+            scale_on_vector(m, GE, VE)
+            scale_on_scalar(m, VE, 4096)
+            store(m, 2048 - m, 4097)
 
-        def norm_clamp(m):
-            ncl = small.tile([P, 1], F32, name="ncl")
-            nc.vector.tensor_scalar(
-                out=ncl[:], in0=n2_t[m][:], scalar1=rn_t[m][:, 0:1], scalar2=20.0,
-                op0=ALU.mult, op1=ALU.min,
-            )
-            ncl_t[m] = ncl
-
-        def norm_exp(m):
-            ep = small.tile([P, 1], F32, name="ep")
-            nc.scalar.activation(out=ep[:], in_=ncl_t[m][:], func=ACT.Exp, scale=0.5)
-            em = small.tile([P, 1], F32, name="em")
-            nc.scalar.activation(out=em[:], in_=ncl_t[m][:], func=ACT.Exp, scale=-0.5)
-            ep_t[m] = ep
-            em_t[m] = em
-
-        def norm_end(m):
-            sc = small.tile([P, 1], F32, name="sc")
-            nc.vector.scalar_tensor_tensor(
-                out=sc[:], in0=ep_t[m][:], scalar=em_t[m][:, 0:1], in1=rn_t[m][:],
-                op0=ALU.subtract, op1=ALU.mult,
-            )
-            nc.vector.tensor_scalar(
-                out=ot_t[m][:, OPAD - 1 : OPAD], in0=ep_t[m][:],
-                scalar1=em_t[m][:, 0:1], scalar2=0.5, op0=ALU.add, op1=ALU.mult,
-            )
-            sc_t[m] = sc
-
-        load_w(0)
-        load_x(0)
-        load_w(1)
-        load_w(2)
-        load_w(3)
-        make_identity(nc, ident_f[:])
-        nc.vector.memset(one[:], 1.0)
-        nc.vector.memset(mhalf[:], -0.5)
-        nc.vector.memset(acc[:], 2e-15)
-        nc.scalar.activation(out=warm[:, 0:1], in_=one[:], func=ACT.Sqrt)
-
-        def bank(m, c):
-            evict(m, c)
-            if m == NT - 1 and c >= NCH - 2:
-                square(m, 512 * c, 512 * (c + 1), c - NCH + 5)
-            elif c % 2 == 1:
-                square(m, 512 * (c - 1), 512 * (c + 1), c // 2)
-
-        for s in range(NCH):
-            transpose_w(s)
-            if XS <= s < XS + len(XSCHED):
-                for m in XSCHED[s - XS]:
-                    transpose_x(m)
-            if s + WBUFS < NCH:
-                load_w(s + WBUFS)
-            if s + WBUFS == NCH - 1:
-                for h in range(4):
-                    load_bias(h)
-            copy_w(s)
-            if s == 0:
-                for m in range(NT):
-                    row_norm(m)
-                    if m == NT - 1:
-                        radicands()
-                roots()
-            if s == 0:
-                factors()
-                quantise_w(0)
-                for m in range(4):
-                    scale_x(m)
-            else:
-                quantise_w(s)
-            if XS <= s < XS + len(XSCHED):
-                for m in XSCHED[s - XS]:
-                    regroup_x(m)
-                for m in XSCHED[s - XS]:
-                    quantise_x(m)
-            if XS <= s < XS + 2:
-                for m in (0, 1):
-                    scale_x(4 + 2 * (s - XS) + m)
-            if s == 3:
-                nc.scalar.activation(out=warm[:, 1:2], in_=one[:], func=ACT.Exp)
-
-        order = [(m, c) for m in range(NT) for c in range(NCH)]
-        last = NT - 1
-        for m, c in order:
-            multiply(m, c)
-            if m >= 1 and c == CLAMP:
-                norm_clamp(m - 1)
-                norm_exp(m - 1)
-            if m >= 1 and c == ROOT:
-                norm_root(m - 1)
-            if m >= 2 and c == Q3:
-                scale_on_gpsimd(m - 2, 2048, GE)
-                scale_on_vector(m - 2, GE, VE)
-                scale_on_scalar(m - 2, VE, 4096)
-                store(m - 2, 2048 - (m - 2), 4097)
-            if m >= 1 and c == (LEND if m == last else END):
-                norm_end(m - 1)
-                scale_on_gpsimd(m - 1, 0, 2048)
-                store(m - 1, 0, 2048 - (m - 1))
-            bank(m, c)
-            if c == NCH - 1:
-                norm_sum(m)
+        for m in range(NT):
+            for c in range(NCH):
+                ps = multiply(m, c)
+                if m >= 1 and c == 3:
+                    norm_exp(m - 1)
+                if m >= 1 and c == 1:
+                    norm_root(m - 1)
+                if m >= 2 and c == 1:
+                    second_half(m - 2)
+                if m >= 1 and c == (5 if m == last else 6):
+                    first_half(m - 1)
+                add_bias(m, c, ps)
+                if m == last and c >= NCH - 2:
+                    square(m, 512 * c, 512 * (c + 1), c - 3)
+                elif c % 2 == 1:
+                    square(m, 512 * (c - 1), 512 * (c + 1), c // 2)
+            norm_sum(m)
 
         m = last
         norm_root(m)
         scale_on_scalar(m - 1, 3072, 4096)
         scale_on_vector(m - 1, 2048, 3072)
         store(m - 1, 2048 - (m - 1), 4097)
-        norm_clamp(m)
         norm_exp(m)
-        norm_end(m)
+        factors(m)
         scale_on_vector(m, 0, 1024)
         store(m, 0, 1024 - m)
         scale_on_vector(m, 1024, 2048)

@@ -23,7 +23,8 @@ X2 = 2080
 OPAD = 8
 WBUFS = 6
 NSUM = 5
-GE, VE = 3328, 3840
+SPLIT = 3328, 3840
+LATE_SPLIT = 2816, 3584
 
 
 def tile_lorentzmlp_pa_kernel(tc, x_hyp, W, b, out):
@@ -52,14 +53,16 @@ def tile_lorentzmlp_pa_kernel(tc, x_hyp, W, b, out):
         bias = const.tile([P, 4096], BF16)
         ident = const.tile([P, P], F32)
         one = const.tile([P, 1], F32)
-        mhalf = const.tile([P, 1], F32)
+        half = const.tile([P, NT], F32)
+        mhalf = const.tile([P, 4], F32)
         warm = const.tile([P, 2], F32)
         acc = const.tile([P, NT * NSUM], F32)
         ss = const.tile([P, NT], F32)
         v = const.tile([P, NT], F32)
         vp1 = const.tile([P, NT], F32)
-        radicand = const.tile([P, 2 * NT], F32)
-        root = const.tile([P, 2 * NT], F32)
+        vsq = const.tile([P, NT], F32)
+        vroot = const.tile([P, NT], F32)
+        ssc = const.tile([P, NT], F32)
         warg = const.tile([P, NT], F32)
         rns = const.tile([P, NT], F32)
         dist = const.tile([P, NT], F32)
@@ -108,24 +111,35 @@ def tile_lorentzmlp_pa_kernel(tc, x_hyp, W, b, out):
                     op0=ALU.mult, op1=ALU.mult, accum_out=ss[:, m : m + 1],
                 )
 
-        def log_map():
+        def time_root():
             nc.vector.tensor_scalar_max(
                 out=v[:].rearrange("p (h j) -> p h j", j=2), in0=xr4[:, :, :, 0],
                 scalar1=1.0 + 1e-7,
             )
             nc.vector.tensor_scalar_add(out=vp1[:], in0=v[:], scalar1=1.0)
             nc.vector.scalar_tensor_tensor(
-                out=radicand[:, NT : 2 * NT], in0=v[:], scalar=-1.0, in1=vp1[:],
-                op0=ALU.add, op1=ALU.mult,
+                out=vsq[:], in0=v[:], scalar=-1.0, in1=vp1[:], op0=ALU.add, op1=ALU.mult
             )
-            nc.vector.tensor_scalar_max(out=radicand[:, 0:NT], in0=ss[:], scalar1=1e-14)
-            nc.scalar.activation(out=root[:], in_=radicand[:], func=ACT.Sqrt)
-            nc.vector.tensor_tensor(
-                out=warg[:], in0=v[:], in1=root[:, NT : 2 * NT], op=ALU.add
-            )
-            nc.vector.reciprocal(out=rns[:], in_=root[:, 0:NT])
+            nc.gpsimd.tensor_tensor(out=vroot[:], in0=vsq[:], in1=half[:], op=ALU.pow)
+
+        def distance():
+            nc.vector.tensor_tensor(out=warg[:], in0=v[:], in1=vroot[:], op=ALU.add)
             nc.scalar.activation(out=dist[:], in_=warg[:], func=ACT.Ln)
-            nc.vector.tensor_tensor(out=sx[:], in0=rns[:], in1=dist[:], op=ALU.mult)
+
+        def inverse_norms(h):
+            lo, hi = 4 * h, 4 * (h + 1)
+            nc.vector.tensor_scalar_max(out=ssc[:, lo:hi], in0=ss[:, lo:hi], scalar1=1e-14)
+            nc.gpsimd.tensor_tensor(
+                out=rns[:, lo:hi], in0=ssc[:, lo:hi], in1=mhalf[:, 0:4], op=ALU.pow
+            )
+
+        def tangent(h):
+            lo, hi = 4 * h, 4 * (h + 1)
+            nc.vector.tensor_tensor(
+                out=sx[:, lo:hi], in0=rns[:, lo:hi], in1=dist[:, lo:hi], op=ALU.mult
+            )
+            for m in range(lo, hi):
+                scale_x(m)
 
         def scale_x(m):
             ts = tpool.tile([P, 1024], BF16, align_bytes=64, name="ts")
@@ -190,30 +204,38 @@ def tile_lorentzmlp_pa_kernel(tc, x_hyp, W, b, out):
                 )
 
         def quantise_w(c):
-            nc.vector.quantize_mx(
-                out=wq[:, c * 1024 : (c + 1) * 1024].bitcast(FP8X4),
-                scales=wsc[:, c * 1024 : (c + 1) * 1024],
-                in_=wg_t[c][:],
-            )
+            parts = 2 if c == NCH - 1 else 1
+            n = 1024 // parts
+            for i in range(parts):
+                lo = c * 1024 + n * i
+                nc.vector.quantize_mx(
+                    out=wq[:, lo : lo + n].bitcast(FP8X4),
+                    scales=wsc[:, lo : lo + n],
+                    in_=wg_t[c][:, 4 * n * i : 4 * n * (i + 1)],
+                )
 
         load_x()
         for c in range(WBUFS):
             load_w(c)
         make_identity(nc, ident[:])
         nc.vector.memset(one[:], 1.0)
+        nc.vector.memset(half[:], 0.5)
         nc.vector.memset(mhalf[:], -0.5)
         nc.vector.memset(acc[:], 2e-15)
-        nc.scalar.activation(out=warm[:, 0:1], in_=one[:], func=ACT.Sqrt)
+        nc.scalar.activation(out=warm[:, 0:1], in_=one[:], func=ACT.Ln)
         for m in range(NT):
+            if m == NT - 1:
+                time_root()
             row_norm(m)
-        log_map()
-        for m in range(NT):
-            scale_x(m)
+        inverse_norms(0)
+        inverse_norms(1)
         for c in range(NCH):
             riders = range(max(0, 2 * c - 5), max(0, min(NT, 2 * c - 3)))
             for tp in range(2):
                 transpose_w(c, tp)
                 copy_w(c, tp)
+                if c == 0 and tp == 1:
+                    distance()
             for m in riders:
                 transpose_x(m)
             if c + WBUFS < NCH:
@@ -221,6 +243,8 @@ def tile_lorentzmlp_pa_kernel(tc, x_hyp, W, b, out):
             if c + WBUFS == NCH - 1:
                 load_bias()
             quantise_w(c)
+            if c <= 1:
+                tangent(c)
             for m in riders:
                 regroup_x(m)
             for m in riders:
@@ -282,7 +306,7 @@ def tile_lorentzmlp_pa_kernel(tc, x_hyp, W, b, out):
 
         def norm_root(m):
             rn = small.tile([P, 1], F32, name="rn")
-            nc.gpsimd.tensor_tensor(out=rn[:], in0=n2_t[m][:], in1=mhalf[:], op=ALU.pow)
+            nc.gpsimd.tensor_tensor(out=rn[:], in0=n2_t[m][:], in1=mhalf[:, 0:1], op=ALU.pow)
             rn_t[m] = rn
 
         def norm_exp(m):
@@ -334,13 +358,17 @@ def tile_lorentzmlp_pa_kernel(tc, x_hyp, W, b, out):
 
         def first_half(m):
             factors(m)
-            scale_on_gpsimd(m, 0, 2048)
+            lo = 512 if m == last - 1 else 0
+            if lo > 0:
+                scale_on_vector(m, 0, lo)
+            scale_on_gpsimd(m, lo, 2048)
             store(m, 0, 2048 - m)
 
         def second_half(m):
-            scale_on_gpsimd(m, 2048, GE)
-            scale_on_vector(m, GE, VE)
-            scale_on_scalar(m, VE, 4096)
+            ge, ve = LATE_SPLIT if m == last - 2 else SPLIT
+            scale_on_gpsimd(m, 2048, ge)
+            scale_on_vector(m, ge, ve)
+            scale_on_scalar(m, ve, 4096)
             store(m, 2048 - m, 4097)
 
         for m in range(NT):

from contextlib import ExitStack

import concourse.mybir as mybir
from concourse.masks import make_identity

FLOPS = 2 * 1024 * 4096 * 1024

F32 = mybir.dt.float32
BF16 = mybir.dt.bfloat16
U32 = mybir.dt.uint32
U8 = mybir.dt.uint8
FP8X4 = mybir.dt.float8_e4m3fn_x4
ALU = mybir.AluOpType
ACT = mybir.ActivationFunctionType

P = 128
NT = 8
NCH = 8
PAD = 32
XP = PAD + 1024
WP = XP // 2
X2 = 2080
OPAD = 8
WBUFS = 6
NSUM = 5
SPLIT = 3328, 3840
LATE_SPLIT = 2816, 3584


def tile_lorentzmlp_pa_kernel(tc, x_hyp, W, b, out):
    nc = tc.nc
    with ExitStack() as ctx:
        ctx.enter_context(tc.manual_schedule())
        const = ctx.enter_context(tc.tile_pool(name="const", bufs=1))
        wpool = ctx.enter_context(tc.tile_pool(name="wraw", bufs=WBUFS))
        gpool = ctx.enter_context(tc.tile_pool(name="grouped", bufs=2))
        tpool = ctx.enter_context(tc.tile_pool(name="ts", bufs=NT))
        spool = ctx.enter_context(tc.tile_pool(name="scratch", bufs=2))
        opool = ctx.enter_context(tc.tile_pool(name="outs", bufs=4))
        small = ctx.enter_context(tc.tile_pool(name="small", bufs=3))
        psum = ctx.enter_context(tc.psum_pool(name="psum", bufs=8))

        xraw = const.tile([P, NT // 2 * X2], BF16, align_bytes=64)
        xpair = xraw[:].rearrange("p (h r) -> p h r", r=X2)[:, :, 0 : 2 * 1025]
        xr4 = xpair.rearrange("p h (j c) -> p h j c", c=1025)
        xsrc = x_hyp.rearrange("(p m) c -> p (m c)", m=NT)
        wsrc = W[1:4097, :].rearrange("(c t p) k -> c p t k", t=4, p=P)
        odst = out.rearrange("(p m) c -> m p c", m=NT)
        xq = const.tile([P, NT * 256], U32, align_bytes=64)
        xsc = const.tile([P, NT * 256], U8, align_bytes=64)
        wq = const.tile([P, NCH * 1024], U32, align_bytes=64)
        wsc = const.tile([P, NCH * 1024], U8, align_bytes=64)
        bias = const.tile([P, 4096], BF16)
        ident = const.tile([P, P], F32)
        one = const.tile([P, 1], F32)
        half = const.tile([P, NT], F32)
        mhalf = const.tile([P, 4], F32)
        warm = const.tile([P, 2], F32)
        acc = const.tile([P, NT * NSUM], F32)
        ss = const.tile([P, NT], F32)
        v = const.tile([P, NT], F32)
        vp1 = const.tile([P, NT], F32)
        vsq = const.tile([P, NT], F32)
        vroot = const.tile([P, NT], F32)
        ssc = const.tile([P, NT], F32)
        warg = const.tile([P, NT], F32)
        rns = const.tile([P, NT], F32)
        dist = const.tile([P, NT], F32)
        sx = const.tile([P, NT], F32)

        wraw_t = {}
        wbank = {}
        wg_t = {}
        ts_t = {}
        xbank = {}
        xg_t = {}

        def load_x():
            for h in range(NT // 2):
                nc.sync.dma_start(
                    out=xpair[:, h, :], in_=xsrc[:, 2050 * h : 2050 * (h + 1)]
                )

        def load_w(c):
            wraw = wpool.tile([P, 4 * XP], BF16, align_bytes=64, name="wraw")
            dst = wraw[:].rearrange("p (t k) -> p t k", k=XP)
            for tp in range(2):
                nc.sync.dma_start(
                    out=dst[:, 2 * tp : 2 * tp + 2, PAD:XP],
                    in_=wsrc[c][:, 2 * tp : 2 * tp + 2, 1:1025],
                )
            wraw_t[c] = wraw

        def load_bias():
            for h in range(4):
                nc.sync.dma_start(
                    out=bias[:, 1024 * h : 1024 * (h + 1)],
                    in_=b[1 + 1024 * h : 1 + 1024 * (h + 1)].partition_broadcast(P),
                )

        def row_norm(m):
            xs = xr4[:, m // 2, m % 2, 1:1025]
            junk = spool.tile([P, 1024], BF16, name="junk" if m % 2 == 0 else "junkv")
            if m % 2 == 0:
                nc.scalar.activation(
                    out=junk[:], in_=xs, func=ACT.Square, accum_out=ss[:, m : m + 1]
                )
            else:
                nc.vector.scalar_tensor_tensor(
                    out=junk[:], in0=xs, scalar=1.0, in1=xs,
                    op0=ALU.mult, op1=ALU.mult, accum_out=ss[:, m : m + 1],
                )

        def time_root():
            nc.vector.tensor_scalar_max(
                out=v[:].rearrange("p (h j) -> p h j", j=2), in0=xr4[:, :, :, 0],
                scalar1=1.0 + 1e-7,
            )
            nc.vector.tensor_scalar_add(out=vp1[:], in0=v[:], scalar1=1.0)
            nc.vector.scalar_tensor_tensor(
                out=vsq[:], in0=v[:], scalar=-1.0, in1=vp1[:], op0=ALU.add, op1=ALU.mult
            )
            nc.gpsimd.tensor_tensor(out=vroot[:], in0=vsq[:], in1=half[:], op=ALU.pow)

        def distance():
            nc.vector.tensor_tensor(out=warg[:], in0=v[:], in1=vroot[:], op=ALU.add)
            nc.scalar.activation(out=dist[:], in_=warg[:], func=ACT.Ln)

        def inverse_norms(h):
            lo, hi = 4 * h, 4 * (h + 1)
            nc.vector.tensor_scalar_max(out=ssc[:, lo:hi], in0=ss[:, lo:hi], scalar1=1e-14)
            nc.gpsimd.tensor_tensor(
                out=rns[:, lo:hi], in0=ssc[:, lo:hi], in1=mhalf[:, 0:4], op=ALU.pow
            )

        def tangent(h):
            lo, hi = 4 * h, 4 * (h + 1)
            nc.vector.tensor_tensor(
                out=sx[:, lo:hi], in0=rns[:, lo:hi], in1=dist[:, lo:hi], op=ALU.mult
            )
            for m in range(lo, hi):
                scale_x(m)

        def scale_x(m):
            ts = tpool.tile([P, 1024], BF16, align_bytes=64, name="ts")
            nc.vector.tensor_scalar(
                out=ts[:], in0=xr4[:, m // 2, m % 2, 1:1025], scalar1=sx[:, m : m + 1],
                scalar2=None, op0=ALU.mult,
            )
            ts_t[m] = ts

        def transpose_x(m):
            xt = psum.tile([P, 512], F32, tag="bank", name="xt")
            words = ts_t[m][:].bitcast(F32)
            for g in range(2):
                for u in range(2):
                    col = (g * 2 + u) * P
                    nc.tensor.transpose(
                        xt[:, col : col + P], words[:, 256 * g + u : 256 * (g + 1) : 2], ident[:]
                    )
            xbank[m] = xt

        def regroup_x(m):
            xg = gpool.tile([P, 1024], BF16, align_bytes=64, name="xg")
            dst = xg[:].bitcast(F32).rearrange("p (g r u) -> p g r u", g=2, u=2)
            src = xbank[m][:].rearrange("p (g u r) -> p g r u", g=2, u=2)
            if m % 2 == 0:
                nc.vector.tensor_copy(out=dst, in_=src)
            else:
                nc.scalar.copy(out=dst, in_=src)
            xg_t[m] = xg

        def quantise_x(m):
            nc.vector.quantize_mx(
                out=xq[:, m * 256 : (m + 1) * 256].bitcast(FP8X4),
                scales=xsc[:, m * 256 : (m + 1) * 256],
                in_=xg_t[m][:],
            )

        def transpose_w(c, tp):
            wf = wraw_t[c][:].bitcast(F32)
            for g in range(2):
                wt = psum.tile([P, 512], F32, tag="bank", name="wt")
                for tl in range(2):
                    for u in range(2):
                        col = (tl * 2 + u) * P
                        src = (2 * tp + tl) * WP + PAD // 2 + 256 * g
                        nc.tensor.transpose(
                            wt[:, col : col + P], wf[:, src + u : src + 256 : 2], ident[:]
                        )
                wbank[(c, 2 * g + tp)] = wt

        def copy_w(c, tp):
            if tp == 0:
                wg = gpool.tile([P, 4096], BF16, align_bytes=64, name="wg")
                wg_t[c] = wg
            wgf = wg_t[c][:].bitcast(F32)
            for k in (tp, 2 + tp):
                nc.scalar.copy(
                    out=wgf[:, k * 512 : (k + 1) * 512].rearrange(
                        "p (tl n u) -> p tl n u", tl=2, u=2
                    ),
                    in_=wbank[(c, k)][:].rearrange("p (tl u n) -> p tl n u", tl=2, u=2),
                )

        def quantise_w(c):
            parts = 2 if c == NCH - 1 else 1
            n = 1024 // parts
            for i in range(parts):
                lo = c * 1024 + n * i
                nc.vector.quantize_mx(
                    out=wq[:, lo : lo + n].bitcast(FP8X4),
                    scales=wsc[:, lo : lo + n],
                    in_=wg_t[c][:, 4 * n * i : 4 * n * (i + 1)],
                )

        load_x()
        for c in range(WBUFS):
            load_w(c)
        make_identity(nc, ident[:])
        nc.vector.memset(one[:], 1.0)
        nc.vector.memset(half[:], 0.5)
        nc.vector.memset(mhalf[:], -0.5)
        nc.vector.memset(acc[:], 2e-15)
        nc.scalar.activation(out=warm[:, 0:1], in_=one[:], func=ACT.Ln)
        for m in range(NT):
            if m == NT - 1:
                time_root()
            row_norm(m)
        inverse_norms(0)
        inverse_norms(1)
        for c in range(NCH):
            riders = range(max(0, 2 * c - 5), max(0, min(NT, 2 * c - 3)))
            for tp in range(2):
                transpose_w(c, tp)
                copy_w(c, tp)
                if c == 0 and tp == 1:
                    distance()
            for m in riders:
                transpose_x(m)
            if c + WBUFS < NCH:
                load_w(c + WBUFS)
            if c + WBUFS == NCH - 1:
                load_bias()
            quantise_w(c)
            if c <= 1:
                tangent(c)
            for m in riders:
                regroup_x(m)
            for m in riders:
                quantise_x(m)
        nc.scalar.activation(out=warm[:, 1:2], in_=one[:], func=ACT.Exp)

        last = NT - 1
        ot_t = {}
        n2_t = {}
        rn_t = {}
        ncl_t = {}
        ep_t = {}
        em_t = {}
        sc_t = {}

        def columns(m, lo, hi):
            return ot_t[m][:, OPAD + lo : OPAD + hi]

        def multiply(m, c):
            ps = psum.tile([P, 512], F32, tag="bank", name="ps")
            for g in range(2):
                lo = (2 * m + g) * P
                ro = c * 1024 + g * 512
                nc.tensor.matmul_mx(
                    out=ps[:],
                    lhsT=xq[:, lo : lo + P].bitcast(FP8X4),
                    lhsT_scale=xsc[:, lo : lo + P],
                    rhs=wq[:, ro : ro + 512].bitcast(FP8X4),
                    rhs_scale=wsc[:, ro : ro + 512],
                    start=(g == 0),
                    stop=(g == 1),
                )
            return ps

        def add_bias(m, c, ps):
            if c == 0:
                ot = opool.tile([P, OPAD + 4096], F32, name="ot")
                ot_t[m] = ot
            nc.vector.tensor_tensor(
                out=columns(m, 512 * c, 512 * (c + 1)), in0=ps[:],
                in1=bias[:, 512 * c : 512 * (c + 1)], op=ALU.add,
            )

        def square(m, lo, hi, j):
            junk = spool.tile([P, 1024], BF16, name="junk")
            nc.scalar.activation(
                out=junk[:, 0 : hi - lo], in_=columns(m, lo, hi), func=ACT.Square,
                accum_out=acc[:, NSUM * m + j : NSUM * m + j + 1],
            )

        def norm_sum(m):
            n2 = small.tile([P, 1], F32, name="n2")
            junk5 = small.tile([P, NSUM], F32, name="junk5")
            nc.scalar.activation(
                out=junk5[:], in_=acc[:, NSUM * m : NSUM * (m + 1)], func=ACT.Copy,
                scale=4.0, accum_out=n2[:],
            )
            n2_t[m] = n2

        def norm_root(m):
            rn = small.tile([P, 1], F32, name="rn")
            nc.gpsimd.tensor_tensor(out=rn[:], in0=n2_t[m][:], in1=mhalf[:, 0:1], op=ALU.pow)
            rn_t[m] = rn

        def norm_exp(m):
            ncl = small.tile([P, 1], F32, name="ncl")
            nc.vector.tensor_scalar(
                out=ncl[:], in0=n2_t[m][:], scalar1=rn_t[m][:, 0:1], scalar2=20.0,
                op0=ALU.mult, op1=ALU.min,
            )
            ep = small.tile([P, 1], F32, name="ep")
            nc.scalar.activation(out=ep[:], in_=ncl[:], func=ACT.Exp, scale=0.5)
            em = small.tile([P, 1], F32, name="em")
            nc.scalar.activation(out=em[:], in_=ncl[:], func=ACT.Exp, scale=-0.5)
            ep_t[m] = ep
            em_t[m] = em

        def factors(m):
            sc = small.tile([P, 1], F32, name="sc")
            nc.vector.scalar_tensor_tensor(
                out=sc[:], in0=ep_t[m][:], scalar=em_t[m][:, 0:1], in1=rn_t[m][:],
                op0=ALU.subtract, op1=ALU.mult,
            )
            nc.gpsimd.tensor_scalar(
                out=ot_t[m][:, OPAD - 1 : OPAD], in0=ep_t[m][:],
                scalar1=em_t[m][:, 0:1], scalar2=0.5, op0=ALU.add, op1=ALU.mult,
            )
            sc_t[m] = sc

        def scale_on_gpsimd(m, lo, hi):
            seg = columns(m, lo, hi)
            nc.gpsimd.tensor_scalar(
                out=seg, in0=seg, scalar1=sc_t[m][:, 0:1], scalar2=0.0,
                op0=ALU.mult, op1=ALU.add,
            )

        def scale_on_vector(m, lo, hi):
            seg = columns(m, lo, hi)
            nc.vector.tensor_scalar(
                out=seg, in0=seg, scalar1=sc_t[m][:, 0:1], scalar2=None, op0=ALU.mult
            )

        def scale_on_scalar(m, lo, hi):
            seg = columns(m, lo, hi)
            nc.scalar.activation(out=seg, in_=seg, func=ACT.Copy, scale=sc_t[m][:, 0:1])

        def store(m, lo, hi):
            nc.sync.dma_start(
                out=odst[m][:, lo:hi], in_=ot_t[m][:, OPAD - 1 + lo : OPAD - 1 + hi]
            )

        def first_half(m):
            factors(m)
            lo = 512 if m == last - 1 else 0
            if lo > 0:
                scale_on_vector(m, 0, lo)
            scale_on_gpsimd(m, lo, 2048)
            store(m, 0, 2048 - m)

        def second_half(m):
            ge, ve = LATE_SPLIT if m == last - 2 else SPLIT
            scale_on_gpsimd(m, 2048, ge)
            scale_on_vector(m, ge, ve)
            scale_on_scalar(m, ve, 4096)
            store(m, 2048 - m, 4097)

        for m in range(NT):
            for c in range(NCH):
                ps = multiply(m, c)
                if m >= 1 and c == 3:
                    norm_exp(m - 1)
                if m >= 1 and c == 1:
                    norm_root(m - 1)
                if m >= 2 and c == 1:
                    second_half(m - 2)
                if m >= 1 and c == (5 if m == last else 6):
                    first_half(m - 1)
                add_bias(m, c, ps)
                if m == last and c >= NCH - 2:
                    square(m, 512 * c, 512 * (c + 1), c - 3)
                elif c % 2 == 1:
                    square(m, 512 * (c - 1), 512 * (c + 1), c // 2)
            norm_sum(m)

        m = last
        norm_root(m)
        scale_on_scalar(m - 1, 3072, 4096)
        scale_on_vector(m - 1, 2048, 3072)
        store(m - 1, 2048 - (m - 1), 4097)
        norm_exp(m)
        factors(m)
        scale_on_vector(m, 0, 1024)
        store(m, 0, 1024 - m)
        scale_on_vector(m, 1024, 2048)
        store(m, 1024 - m, 2048 - m)
        scale_on_scalar(m, 2048, 3072)
        store(m, 2048 - m, 3072 - m)
        scale_on_vector(m, 3072, 4096)
        store(m, 3072 - m, 4097)
